import numpy as np
import ml_dtypes

BF16 = ml_dtypes.bfloat16


def bf(x):
    return np.asarray(x, np.float32).astype(BF16)


def f32(x):
    return np.asarray(x, np.float32)


def f64(x):
    return np.asarray(x).astype(np.float64)


def striped(idx):
    return np.tile(idx.reshape(-1, 16).T, (8, 1))


F, C, S, N, LP = 512, 512, 2048, 1024, 2
LAMDA, ALPHA, EDGE_P, WSCALE = 0.5, 0.1, 0.016, 3.0


def setup_inputs():
    x = bf(np.random.standard_normal((F, N)))
    up = np.triu((np.random.random((N, N)) < EDGE_P).astype(np.float32), 1)
    adj = bf(up + up.T)
    fc1_w = bf(np.random.standard_normal((F, C)) / np.sqrt(C))
    fc1_b = f32(0.1 * np.random.standard_normal((C, 1)))
    conv_w = bf(np.random.uniform(-WSCALE / np.sqrt(C), WSCALE / np.sqrt(C), (LP, C, C)))
    base = f32(0.5 * np.random.standard_normal((C, S)))
    return {"x": x, "adj": adj, "fc1_w": fc1_w, "fc1_b": fc1_b, "conv_w": conv_w, "base": base, "offs": striped(np.random.permutation(S)[:N])}


def reference(x, adj, fc1_w, fc1_b, conv_w, base, offs):
    idx = offs[:16].T.reshape(-1)
    a_hat = f64(adj) + np.eye(N)
    dinv = 1.0 / np.sqrt(a_hat.sum(axis=0))
    p_t = (dinv[:, None] * a_hat * dinv[None, :]).T
    h0 = np.maximum(f64(fc1_w).T @ f64(x) + f64(fc1_b), 0.0)
    h = h0
    for t in range(LP):
        beta = np.log(LAMDA / (t + 1) + 1.0)
        r = (1.0 - ALPHA) * (h @ p_t) + ALPHA * h0
        h = np.maximum((1.0 - beta) * r + beta * (f64(conv_w[t]).T @ r), 0.0)
    out = f64(base).copy()
    out[:, idx] = (1.0 - ALPHA) * (h @ p_t) + ALPHA * h0
    return out

@@ -1,0 +1,169 @@
+import math
+
+import concourse.mybir as mybir
+from concourse.masks import make_identity
+
+F32, BF16, U16 = mybir.dt.float32, mybir.dt.bfloat16, mybir.dt.uint16
+ALU = mybir.AluOpType
+ACT = mybir.ActivationFunctionType
+
+P = 128
+F, C, S, N = 512, 512, 2048, 1024
+LAYERS = 2
+ALPHA, LAMDA = 0.1, 0.5
+BANK = 512
+F_BLOCKS, C_BLOCKS, N_BLOCKS = F // P, C // P, N // P
+HALVES = N // BANK
+
+FLOPS = 2 * N * (F * C + LAYERS * C * C + (LAYERS + 1) * C * N)
+
+
+def half(h):
+    return slice(h * BANK, (h + 1) * BANK)
+
+
+def block(b):
+    return slice(b * P, (b + 1) * P)
+
+
+def tile_gcnii_b_kernel(tc, x, adj, fc1_w, fc1_b, conv_w, base, offs, out):
+    nc = tc.nc
+    with (
+        tc.tile_pool(name="lists", bufs=1) as lists,
+        tc.tile_pool(name="held", bufs=1) as held,
+        tc.tile_pool(name="layer", bufs=2) as layer,
+        tc.tile_pool(name="work", bufs=3) as work,
+        tc.psum_pool(name="banks", bufs=6) as banks,
+        tc.psum_pool(name="flips", bufs=2) as flips,
+    ):
+        offsets = lists.tile([P, N // 16], U16, name="offsets")
+        nc.sync.dma_start(offsets[:], offs)
+
+        adj_sb = held.tile([P, N_BLOCKS, N], BF16, name="adj_sb")
+        for kb in range(N_BLOCKS):
+            nc.sync.dma_start(adj_sb[:, kb, :], adj[block(kb), :])
+        fc1_w_sb = held.tile([P, F_BLOCKS, C], BF16, name="fc1_w_sb")
+        nc.sync.dma_start(fc1_w_sb[:], fc1_w.rearrange("(fb p) c -> p fb c", p=P))
+        x_sb = held.tile([P, F_BLOCKS, N], BF16, name="x_sb")
+        for fb in range(F_BLOCKS):
+            nc.sync.dma_start(x_sb[:, fb, :], x[block(fb), :])
+        conv_w_sb = held.tile([P, LAYERS, C_BLOCKS, C], BF16, name="conv_w_sb")
+        for t in range(LAYERS):
+            nc.sync.dma_start(conv_w_sb[:, t], conv_w[t].rearrange("(cb p) d -> p cb d", p=P))
+        windows = [held.tile([P, S], F32, name=f"window{cb}") for cb in range(C_BLOCKS)]
+        for cb in range(C_BLOCKS):
+            nc.sync.dma_start(windows[cb][:], base[block(cb), :])
+        bias = held.tile([P, C_BLOCKS], F32, name="bias")
+        with nc.allow_non_contiguous_dma(reason="512 bias values, one to a partition"):
+            nc.gpsimd.dma_start(bias[:], fc1_b.rearrange("(cb p) one -> p (cb one)", p=P))
+
+        identity = held.tile([P, P], BF16, name="identity")
+        make_identity(nc, identity[:])
+        ones = held.tile([P, P], BF16, name="ones")
+        nc.vector.memset(ones[:], 1.0)
+        bias_tenth = held.tile([P, C_BLOCKS], F32, name="bias_tenth")
+        nc.gpsimd.tensor_scalar_mul(bias_tenth[:], bias[:], ALPHA)
+
+        column_sums = [banks.tile([P, BANK], F32, name=f"column_sums{h}", tag="bank") for h in range(HALVES)]
+        row_sums = [held.tile([P, N_BLOCKS // 2], F32, name=f"row_sums{parity}") for parity in range(2)]
+        for kb in range(N_BLOCKS):
+            for h in range(HALVES):
+                nc.tensor.matmul(
+                    column_sums[h][:], ones[:], adj_sb[:, kb, half(h)], start=(kb == 0), stop=(kb == N_BLOCKS - 1)
+                )
+            row_sum = row_sums[kb % 2][:, kb // 2 : kb // 2 + 1]
+            if kb % 2 == 0:
+                nc.vector.reduce_sum(row_sum, adj_sb[:, kb, :], axis=mybir.AxisListType.X)
+            else:
+                unused = work.tile([P, N], BF16, name="unused")
+                nc.scalar.activation(unused[:], adj_sb[:, kb, :], ACT.Copy, accum_out=row_sum)
+            nc.gpsimd.tensor_tensor(adj_sb[:, kb, block(kb)], adj_sb[:, kb, block(kb)], identity[:], ALU.add)
+
+        dinv_free = held.tile([P, N], F32, name="dinv_free")
+        for h in range(HALVES):
+            nc.scalar.activation(dinv_free[:, half(h)], column_sums[h][:], ACT.Abs_reciprocal_sqrt, bias=1.0)
+        dinv_part = [held.tile([P, N_BLOCKS // 2], F32, name=f"dinv_part{parity}") for parity in range(2)]
+        for parity in range(2):
+            nc.scalar.activation(dinv_part[parity][:], row_sums[parity][:], ACT.Abs_reciprocal_sqrt, bias=1.0)
+
+        p_sb = held.tile([P, N_BLOCKS, N], BF16, name="p_sb")
+        for h in range(HALVES):
+            for kb in range(N_BLOCKS):
+                nc.vector.scalar_tensor_tensor(
+                    p_sb[:, kb, half(h)],
+                    adj_sb[:, kb, half(h)],
+                    dinv_part[kb % 2][:, kb // 2 : kb // 2 + 1],
+                    dinv_free[:, half(h)],
+                    ALU.mult,
+                    ALU.mult,
+                )
+
+        h0_tenth = [held.tile([P, N], F32, name=f"h0_tenth{cb}") for cb in range(C_BLOCKS)]
+        r_bf16 = None
+        r_kept = None
+        for t in range(LAYERS + 1):
+            beta = math.log(LAMDA / t + 1.0) if t > 0 else None
+            beta_next = math.log(LAMDA / (t + 1) + 1.0)
+            r_bf16_next, r_kept_next = [], []
+            for cb in range(C_BLOCKS):
+                product = [banks.tile([P, BANK], F32, name=f"product{h}", tag="bank") for h in range(HALVES)]
+                for ib in range(C_BLOCKS):
+                    for h in range(HALVES):
+                        if t == 0:
+                            weights, moving = fc1_w_sb[:, ib, block(cb)], x_sb[:, ib, half(h)]
+                        else:
+                            weights, moving = conv_w_sb[:, t - 1, ib, block(cb)], r_bf16[ib][:, half(h)]
+                        nc.tensor.matmul(
+                            product[h][:], weights, moving, start=(ib == 0), stop=(ib == C_BLOCKS - 1)
+                        )
+
+                pre = work.tile([P, N], BF16, name="pre")
+                for h in range(HALVES):
+                    if t == 0:
+                        nc.scalar.activation(pre[:, half(h)], product[h][:], ACT.Identity, bias=bias[:, cb : cb + 1])
+                        nc.scalar.activation(
+                            h0_tenth[cb][:, half(h)],
+                            product[h][:],
+                            ACT.Relu,
+                            bias=bias_tenth[:, cb : cb + 1],
+                            scale=ALPHA,
+                        )
+                    else:
+                        nc.vector.scalar_tensor_tensor(
+                            pre[:, half(h)], product[h][:], beta, r_kept[cb][:, half(h)], ALU.mult, ALU.add
+                        )
+
+                flipped = flips.tile([P, N], BF16, name="flipped")
+                for kb in range(N_BLOCKS):
+                    nc.tensor.transpose(flipped[:, block(kb)], pre[:, block(kb)], identity[:])
+                h_nodes = work.tile([P, N], BF16, name="h_nodes")
+                nc.scalar.activation(h_nodes[:], flipped[:], ACT.Relu)
+
+                spread = [banks.tile([P, BANK], F32, name=f"spread{h}", tag="bank") for h in range(HALVES)]
+                for kb in range(N_BLOCKS):
+                    for h in range(HALVES):
+                        nc.tensor.matmul(
+                            spread[h][:],
+                            h_nodes[:, block(kb)],
+                            p_sb[:, kb, half(h)],
+                            start=(kb == 0),
+                            stop=(kb == N_BLOCKS - 1),
+                        )
+
+                if t < LAYERS:
+                    r = work.tile([P, N], F32, name="r")
+                    r_bf16_next.append(layer.tile([P, N], BF16, name=f"r_bf16_{cb}"))
+                    r_kept_next.append(layer.tile([P, N], F32, name=f"r_kept_{cb}"))
+                    for h in range(HALVES):
+                        nc.vector.scalar_tensor_tensor(
+                            r[:, half(h)], spread[h][:], 1.0 - ALPHA, h0_tenth[cb][:, half(h)], ALU.mult, ALU.add
+                        )
+                        nc.scalar.copy(r_bf16_next[cb][:, half(h)], r[:, half(h)])
+                        nc.gpsimd.tensor_scalar_mul(r_kept_next[cb][:, half(h)], r[:, half(h)], 1.0 - beta_next)
+                else:
+                    term = work.tile([P, N], F32, name="term")
+                    for h in range(HALVES):
+                        nc.scalar.mul(term[:, half(h)], spread[h][:], 1.0 - ALPHA)
+                    nc.vector.tensor_tensor(windows[cb][:].indirect(offsets[:]), term[:], h0_tenth[cb][:], ALU.add)
+                    nc.sync.dma_start(out[block(cb), :], windows[cb][:])
+            r_bf16, r_kept = r_bf16_next, r_kept_next

@@ -99,71 +99,74 @@ def tile_gcnii_b_kernel(tc, x, adj, fc1_w, fc1_b, conv_w, base, offs, out):
                 )
 
         h0_tenth = [held.tile([P, N], F32, name=f"h0_tenth{cb}") for cb in range(C_BLOCKS)]
-        r_bf16 = None
-        r_kept = None
-        for t in range(LAYERS + 1):
-            beta = math.log(LAMDA / t + 1.0) if t > 0 else None
-            beta_next = math.log(LAMDA / (t + 1) + 1.0)
-            r_bf16_next, r_kept_next = [], []
-            for cb in range(C_BLOCKS):
-                product = [banks.tile([P, BANK], F32, name=f"product{h}", tag="bank") for h in range(HALVES)]
+        pre = {}
+        h_nodes = {}
+        r_bf16 = {}
+        r_kept = {}
+
+        def weigh(t, cb):
+            pre[cb] = work.tile([P, N], BF16, name="pre")
+            for h in range(HALVES):
+                product = banks.tile([P, BANK], F32, name="product", tag="bank")
                 for ib in range(C_BLOCKS):
-                    for h in range(HALVES):
-                        if t == 0:
-                            weights, moving = fc1_w_sb[:, ib, block(cb)], x_sb[:, ib, half(h)]
-                        else:
-                            weights, moving = conv_w_sb[:, t - 1, ib, block(cb)], r_bf16[ib][:, half(h)]
-                        nc.tensor.matmul(
-                            product[h][:], weights, moving, start=(ib == 0), stop=(ib == C_BLOCKS - 1)
-                        )
-
-                pre = work.tile([P, N], BF16, name="pre")
-                for h in range(HALVES):
                     if t == 0:
-                        nc.scalar.activation(pre[:, half(h)], product[h][:], ACT.Identity, bias=bias[:, cb : cb + 1])
-                        nc.scalar.activation(
-                            h0_tenth[cb][:, half(h)],
-                            product[h][:],
-                            ACT.Relu,
-                            bias=bias_tenth[:, cb : cb + 1],
-                            scale=ALPHA,
-                        )
+                        weights, moving = fc1_w_sb[:, ib, block(cb)], x_sb[:, ib, half(h)]
                     else:
-                        nc.vector.scalar_tensor_tensor(
-                            pre[:, half(h)], product[h][:], beta, r_kept[cb][:, half(h)], ALU.mult, ALU.add
-                        )
-
-                flipped = flips.tile([P, N], BF16, name="flipped")
-                for kb in range(N_BLOCKS):
-                    nc.tensor.transpose(flipped[:, block(kb)], pre[:, block(kb)], identity[:])
-                h_nodes = work.tile([P, N], BF16, name="h_nodes")
-                nc.scalar.activation(h_nodes[:], flipped[:], ACT.Relu)
-
-                spread = [banks.tile([P, BANK], F32, name=f"spread{h}", tag="bank") for h in range(HALVES)]
-                for kb in range(N_BLOCKS):
-                    for h in range(HALVES):
-                        nc.tensor.matmul(
-                            spread[h][:],
-                            h_nodes[:, block(kb)],
-                            p_sb[:, kb, half(h)],
-                            start=(kb == 0),
-                            stop=(kb == N_BLOCKS - 1),
-                        )
-
-                if t < LAYERS:
-                    r = work.tile([P, N], F32, name="r")
-                    r_bf16_next.append(layer.tile([P, N], BF16, name=f"r_bf16_{cb}"))
-                    r_kept_next.append(layer.tile([P, N], F32, name=f"r_kept_{cb}"))
-                    for h in range(HALVES):
-                        nc.vector.scalar_tensor_tensor(
-                            r[:, half(h)], spread[h][:], 1.0 - ALPHA, h0_tenth[cb][:, half(h)], ALU.mult, ALU.add
-                        )
-                        nc.scalar.copy(r_bf16_next[cb][:, half(h)], r[:, half(h)])
-                        nc.gpsimd.tensor_scalar_mul(r_kept_next[cb][:, half(h)], r[:, half(h)], 1.0 - beta_next)
+                        weights, moving = conv_w_sb[:, t - 1, ib, block(cb)], r_bf16[t - 1, ib][:, half(h)]
+                    nc.tensor.matmul(product[:], weights, moving, start=(ib == 0), stop=(ib == C_BLOCKS - 1))
+                if t == 0:
+                    nc.scalar.activation(pre[cb][:, half(h)], product[:], ACT.Identity, bias=bias[:, cb : cb + 1])
+                    nc.scalar.activation(
+                        h0_tenth[cb][:, half(h)], product[:], ACT.Relu, bias=bias_tenth[:, cb : cb + 1], scale=ALPHA
+                    )
                 else:
-                    term = work.tile([P, N], F32, name="term")
-                    for h in range(HALVES):
-                        nc.scalar.mul(term[:, half(h)], spread[h][:], 1.0 - ALPHA)
-                    nc.vector.tensor_tensor(windows[cb][:].indirect(offsets[:]), term[:], h0_tenth[cb][:], ALU.add)
-                    nc.sync.dma_start(out[block(cb), :], windows[cb][:])
-            r_bf16, r_kept = r_bf16_next, r_kept_next
+                    beta = math.log(LAMDA / t + 1.0)
+                    nc.vector.scalar_tensor_tensor(
+                        pre[cb][:, half(h)], product[:], beta, r_kept[t - 1, cb][:, half(h)], ALU.mult, ALU.add
+                    )
+
+        def flip(cb):
+            flipped = flips.tile([P, N], BF16, name="flipped")
+            for kb in range(N_BLOCKS):
+                nc.tensor.transpose(flipped[:, block(kb)], pre[cb][:, block(kb)], identity[:])
+            h_nodes[cb] = work.tile([P, N], BF16, name="h_nodes")
+            nc.scalar.activation(h_nodes[cb][:], flipped[:], ACT.Relu)
+
+        def propagate(t, cb):
+            if t < LAYERS:
+                r = work.tile([P, N], F32, name="r")
+                r_bf16[t, cb] = layer.tile([P, N], BF16, name=f"r_bf16_{cb}")
+                r_kept[t, cb] = layer.tile([P, N], F32, name=f"r_kept_{cb}")
+            else:
+                term = work.tile([P, N], F32, name="term")
+            for h in range(HALVES):
+                spread = banks.tile([P, BANK], F32, name="spread", tag="bank")
+                for kb in range(N_BLOCKS):
+                    nc.tensor.matmul(
+                        spread[:],
+                        h_nodes[cb][:, block(kb)],
+                        p_sb[:, kb, half(h)],
+                        start=(kb == 0),
+                        stop=(kb == N_BLOCKS - 1),
+                    )
+                if t < LAYERS:
+                    beta = math.log(LAMDA / (t + 1) + 1.0)
+                    nc.vector.scalar_tensor_tensor(
+                        r[:, half(h)], spread[:], 1.0 - ALPHA, h0_tenth[cb][:, half(h)], ALU.mult, ALU.add
+                    )
+                    nc.scalar.copy(r_bf16[t, cb][:, half(h)], r[:, half(h)])
+                    nc.scalar.mul(r_kept[t, cb][:, half(h)], r[:, half(h)], 1.0 - beta)
+                else:
+                    nc.scalar.mul(term[:, half(h)], spread[:], 1.0 - ALPHA)
+            if t == LAYERS:
+                nc.vector.tensor_tensor(windows[cb][:].indirect(offsets[:]), term[:], h0_tenth[cb][:], ALU.add)
+                nc.sync.dma_start(out[block(cb), :], windows[cb][:])
+
+        for t in range(LAYERS + 1):
+            for step in range(C_BLOCKS + 2):
+                if step < C_BLOCKS:
+                    weigh(t, step)
+                if 1 <= step <= C_BLOCKS:
+                    flip(step - 1)
+                if step >= 2:
+                    propagate(t, step - 2)

@@ -7,23 +7,28 @@ F32, BF16, U16 = mybir.dt.float32, mybir.dt.bfloat16, mybir.dt.uint16
 ALU = mybir.AluOpType
 ACT = mybir.ActivationFunctionType
 
-P = 128
+LANES = 128
 F, C, S, N = 512, 512, 2048, 1024
 LAYERS = 2
 ALPHA, LAMDA = 0.1, 0.5
 BANK = 512
-F_BLOCKS, C_BLOCKS, N_BLOCKS = F // P, C // P, N // P
+C_BLOCKS, N_BLOCKS = C // LANES, N // LANES
 HALVES = N // BANK
+assert F == C
 
 FLOPS = 2 * N * (F * C + LAYERS * C * C + (LAYERS + 1) * C * N)
 
 
-def half(h):
-    return slice(h * BANK, (h + 1) * BANK)
+def beta(t):
+    return math.log(LAMDA / (t + 1) + 1.0)
 
 
 def block(b):
-    return slice(b * P, (b + 1) * P)
+    return slice(b * LANES, (b + 1) * LANES)
+
+
+def half(hf):
+    return slice(hf * BANK, (hf + 1) * BANK)
 
 
 def tile_gcnii_b_kernel(tc, x, adj, fc1_w, fc1_b, conv_w, base, offs, out):
@@ -36,128 +41,123 @@ def tile_gcnii_b_kernel(tc, x, adj, fc1_w, fc1_b, conv_w, base, offs, out):
         tc.psum_pool(name="banks", bufs=6) as banks,
         tc.psum_pool(name="flips", bufs=2) as flips,
     ):
-        offsets = lists.tile([P, N // 16], U16, name="offsets")
+        offsets = lists.tile([LANES, N // 16], U16, name="offsets")
         nc.sync.dma_start(offsets[:], offs)
 
-        adj_sb = held.tile([P, N_BLOCKS, N], BF16, name="adj_sb")
+        adj_sb = held.tile([LANES, N_BLOCKS, N], BF16, name="adj_sb")
         for kb in range(N_BLOCKS):
             nc.sync.dma_start(adj_sb[:, kb, :], adj[block(kb), :])
-        fc1_w_sb = held.tile([P, F_BLOCKS, C], BF16, name="fc1_w_sb")
-        nc.sync.dma_start(fc1_w_sb[:], fc1_w.rearrange("(fb p) c -> p fb c", p=P))
-        x_sb = held.tile([P, F_BLOCKS, N], BF16, name="x_sb")
-        for fb in range(F_BLOCKS):
-            nc.sync.dma_start(x_sb[:, fb, :], x[block(fb), :])
-        conv_w_sb = held.tile([P, LAYERS, C_BLOCKS, C], BF16, name="conv_w_sb")
+        fc1_w_sb = held.tile([LANES, C_BLOCKS, C], BF16, name="fc1_w_sb")
+        nc.sync.dma_start(fc1_w_sb[:], fc1_w.rearrange("(ib p) c -> p ib c", p=LANES))
+        x_sb = held.tile([LANES, C_BLOCKS, N], BF16, name="x_sb")
+        for hf in range(HALVES):
+            nc.sync.dma_start(x_sb[:, :, half(hf)], x[:, half(hf)].rearrange("(ib p) i -> p ib i", p=LANES))
+        conv_w_sb = held.tile([LANES, LAYERS, C_BLOCKS, C], BF16, name="conv_w_sb")
         for t in range(LAYERS):
-            nc.sync.dma_start(conv_w_sb[:, t], conv_w[t].rearrange("(cb p) d -> p cb d", p=P))
-        windows = [held.tile([P, S], F32, name=f"window{cb}") for cb in range(C_BLOCKS)]
+            nc.sync.dma_start(conv_w_sb[:, t], conv_w[t].rearrange("(ib p) d -> p ib d", p=LANES))
+        windows = [held.tile([LANES, S], F32, name=f"window{cb}") for cb in range(C_BLOCKS)]
         for cb in range(C_BLOCKS):
             nc.sync.dma_start(windows[cb][:], base[block(cb), :])
-        bias = held.tile([P, C_BLOCKS], F32, name="bias")
+        bias = held.tile([LANES, C_BLOCKS], F32, name="bias")
         with nc.allow_non_contiguous_dma(reason="512 bias values, one to a partition"):
-            nc.gpsimd.dma_start(bias[:], fc1_b.rearrange("(cb p) one -> p (cb one)", p=P))
+            nc.gpsimd.dma_start(bias[:], fc1_b.rearrange("(cb p) one -> p (cb one)", p=LANES))
 
-        identity = held.tile([P, P], BF16, name="identity")
+        identity = held.tile([LANES, LANES], BF16, name="identity")
         make_identity(nc, identity[:])
-        ones = held.tile([P, P], BF16, name="ones")
+        ones = held.tile([LANES, LANES], BF16, name="ones")
         nc.vector.memset(ones[:], 1.0)
-        bias_tenth = held.tile([P, C_BLOCKS], F32, name="bias_tenth")
+        bias_tenth = held.tile([LANES, C_BLOCKS], F32, name="bias_tenth")
         nc.gpsimd.tensor_scalar_mul(bias_tenth[:], bias[:], ALPHA)
 
-        column_sums = [banks.tile([P, BANK], F32, name=f"column_sums{h}", tag="bank") for h in range(HALVES)]
-        row_sums = [held.tile([P, N_BLOCKS // 2], F32, name=f"row_sums{parity}") for parity in range(2)]
+        column_sums = [banks.tile([LANES, BANK], F32, name=f"column_sums{hf}", tag="bank") for hf in range(HALVES)]
+        row_sums = held.tile([LANES, N_BLOCKS], F32, name="row_sums")
         for kb in range(N_BLOCKS):
-            for h in range(HALVES):
+            for hf in range(HALVES):
                 nc.tensor.matmul(
-                    column_sums[h][:], ones[:], adj_sb[:, kb, half(h)], start=(kb == 0), stop=(kb == N_BLOCKS - 1)
+                    column_sums[hf][:], ones[:], adj_sb[:, kb, half(hf)], start=(kb == 0), stop=(kb == N_BLOCKS - 1)
                 )
-            row_sum = row_sums[kb % 2][:, kb // 2 : kb // 2 + 1]
-            if kb % 2 == 0:
-                nc.vector.reduce_sum(row_sum, adj_sb[:, kb, :], axis=mybir.AxisListType.X)
-            else:
-                unused = work.tile([P, N], BF16, name="unused")
-                nc.scalar.activation(unused[:], adj_sb[:, kb, :], ACT.Copy, accum_out=row_sum)
+            unused = work.tile([LANES, N], BF16, name="unused")
+            nc.vector.tensor_scalar(
+                unused[:], adj_sb[:, kb, :], 1.0, None, ALU.mult, ALU.add, accum_out=row_sums[:, kb : kb + 1]
+            )
             nc.gpsimd.tensor_tensor(adj_sb[:, kb, block(kb)], adj_sb[:, kb, block(kb)], identity[:], ALU.add)
 
-        dinv_free = held.tile([P, N], F32, name="dinv_free")
-        for h in range(HALVES):
-            nc.scalar.activation(dinv_free[:, half(h)], column_sums[h][:], ACT.Abs_reciprocal_sqrt, bias=1.0)
-        dinv_part = [held.tile([P, N_BLOCKS // 2], F32, name=f"dinv_part{parity}") for parity in range(2)]
-        for parity in range(2):
-            nc.scalar.activation(dinv_part[parity][:], row_sums[parity][:], ACT.Abs_reciprocal_sqrt, bias=1.0)
+        dinv_free = held.tile([LANES, N], F32, name="dinv_free")
+        for hf in range(HALVES):
+            nc.scalar.activation(dinv_free[:, half(hf)], column_sums[hf][:], ACT.Abs_reciprocal_sqrt, bias=1.0)
+        dinv_lane = held.tile([LANES, N_BLOCKS], F32, name="dinv_lane")
+        nc.scalar.activation(dinv_lane[:], row_sums[:], ACT.Abs_reciprocal_sqrt, bias=1.0)
 
-        p_sb = held.tile([P, N_BLOCKS, N], BF16, name="p_sb")
-        for h in range(HALVES):
+        p_sb = held.tile([LANES, N_BLOCKS, N], BF16, name="p_sb")
+        for hf in range(HALVES):
             for kb in range(N_BLOCKS):
                 nc.vector.scalar_tensor_tensor(
-                    p_sb[:, kb, half(h)],
-                    adj_sb[:, kb, half(h)],
-                    dinv_part[kb % 2][:, kb // 2 : kb // 2 + 1],
-                    dinv_free[:, half(h)],
+                    p_sb[:, kb, half(hf)],
+                    adj_sb[:, kb, half(hf)],
+                    dinv_lane[:, kb : kb + 1],
+                    dinv_free[:, half(hf)],
                     ALU.mult,
                     ALU.mult,
                 )
 
-        h0_tenth = [held.tile([P, N], F32, name=f"h0_tenth{cb}") for cb in range(C_BLOCKS)]
+        h0_tenth = [held.tile([LANES, N], F32, name=f"h0_tenth{cb}") for cb in range(C_BLOCKS)]
         pre = {}
         h_nodes = {}
         r_bf16 = {}
         r_kept = {}
 
-        def weigh(t, cb):
-            pre[cb] = work.tile([P, N], BF16, name="pre")
-            for h in range(HALVES):
-                product = banks.tile([P, BANK], F32, name="product", tag="bank")
+        def mix_channels(t, cb):
+            pre[cb] = work.tile([LANES, N], BF16, name="pre")
+            for hf in range(HALVES):
+                product = banks.tile([LANES, BANK], F32, name="product", tag="bank")
                 for ib in range(C_BLOCKS):
                     if t == 0:
-                        weights, moving = fc1_w_sb[:, ib, block(cb)], x_sb[:, ib, half(h)]
+                        weights, moving = fc1_w_sb[:, ib, block(cb)], x_sb[:, ib, half(hf)]
                     else:
-                        weights, moving = conv_w_sb[:, t - 1, ib, block(cb)], r_bf16[t - 1, ib][:, half(h)]
+                        weights, moving = conv_w_sb[:, t - 1, ib, block(cb)], r_bf16[t - 1, ib][:, half(hf)]
                     nc.tensor.matmul(product[:], weights, moving, start=(ib == 0), stop=(ib == C_BLOCKS - 1))
                 if t == 0:
-                    nc.scalar.activation(pre[cb][:, half(h)], product[:], ACT.Identity, bias=bias[:, cb : cb + 1])
+                    nc.scalar.activation(pre[cb][:, half(hf)], product[:], ACT.Identity, bias=bias[:, cb : cb + 1])
                     nc.scalar.activation(
-                        h0_tenth[cb][:, half(h)], product[:], ACT.Relu, bias=bias_tenth[:, cb : cb + 1], scale=ALPHA
+                        h0_tenth[cb][:, half(hf)], product[:], ACT.Relu, bias=bias_tenth[:, cb : cb + 1], scale=ALPHA
                     )
                 else:
-                    beta = math.log(LAMDA / t + 1.0)
                     nc.vector.scalar_tensor_tensor(
-                        pre[cb][:, half(h)], product[:], beta, r_kept[t - 1, cb][:, half(h)], ALU.mult, ALU.add
+                        pre[cb][:, half(hf)], product[:], beta(t - 1), r_kept[t - 1, cb][:, half(hf)], ALU.mult, ALU.add
                     )
 
         def flip(cb):
-            flipped = flips.tile([P, N], BF16, name="flipped")
+            flipped = flips.tile([LANES, N], BF16, name="flipped")
             for kb in range(N_BLOCKS):
                 nc.tensor.transpose(flipped[:, block(kb)], pre[cb][:, block(kb)], identity[:])
-            h_nodes[cb] = work.tile([P, N], BF16, name="h_nodes")
+            h_nodes[cb] = work.tile([LANES, N], BF16, name="h_nodes")
             nc.scalar.activation(h_nodes[cb][:], flipped[:], ACT.Relu)
 
         def propagate(t, cb):
             if t < LAYERS:
-                r = work.tile([P, N], F32, name="r")
-                r_bf16[t, cb] = layer.tile([P, N], BF16, name=f"r_bf16_{cb}")
-                r_kept[t, cb] = layer.tile([P, N], F32, name=f"r_kept_{cb}")
+                r = work.tile([LANES, N], F32, name="r")
+                r_bf16[t, cb] = layer.tile([LANES, N], BF16, name=f"r_bf16_{cb}")
+                r_kept[t, cb] = layer.tile([LANES, N], F32, name=f"r_kept_{cb}")
             else:
-                term = work.tile([P, N], F32, name="term")
-            for h in range(HALVES):
-                spread = banks.tile([P, BANK], F32, name="spread", tag="bank")
+                term = work.tile([LANES, N], F32, name="term")
+            for hf in range(HALVES):
+                spread = banks.tile([LANES, BANK], F32, name="spread", tag="bank")
                 for kb in range(N_BLOCKS):
                     nc.tensor.matmul(
                         spread[:],
                         h_nodes[cb][:, block(kb)],
-                        p_sb[:, kb, half(h)],
+                        p_sb[:, kb, half(hf)],
                         start=(kb == 0),
                         stop=(kb == N_BLOCKS - 1),
                     )
                 if t < LAYERS:
-                    beta = math.log(LAMDA / (t + 1) + 1.0)
                     nc.vector.scalar_tensor_tensor(
-                        r[:, half(h)], spread[:], 1.0 - ALPHA, h0_tenth[cb][:, half(h)], ALU.mult, ALU.add
+                        r[:, half(hf)], spread[:], 1.0 - ALPHA, h0_tenth[cb][:, half(hf)], ALU.mult, ALU.add
                     )
-                    nc.scalar.copy(r_bf16[t, cb][:, half(h)], r[:, half(h)])
-                    nc.scalar.mul(r_kept[t, cb][:, half(h)], r[:, half(h)], 1.0 - beta)
+                    nc.scalar.copy(r_bf16[t, cb][:, half(hf)], r[:, half(hf)])
+                    nc.scalar.mul(r_kept[t, cb][:, half(hf)], r[:, half(hf)], 1.0 - beta(t))
                 else:
-                    nc.scalar.mul(term[:, half(h)], spread[:], 1.0 - ALPHA)
+                    nc.scalar.mul(term[:, half(hf)], spread[:], 1.0 - ALPHA)
             if t == LAYERS:
                 nc.vector.tensor_tensor(windows[cb][:].indirect(offsets[:]), term[:], h0_tenth[cb][:], ALU.add)
                 nc.sync.dma_start(out[block(cb), :], windows[cb][:])
@@ -165,8 +165,8 @@ def tile_gcnii_b_kernel(tc, x, adj, fc1_w, fc1_b, conv_w, base, offs, out):
         for t in range(LAYERS + 1):
             for step in range(C_BLOCKS + 2):
                 if step < C_BLOCKS:
-                    weigh(t, step)
+                    mix_channels(t, step)
                 if 1 <= step <= C_BLOCKS:
                     flip(step - 1)
-                if step >= 2:
+                if 2 <= step:
                     propagate(t, step - 2)

@@ -102,11 +102,17 @@ def tile_gcnii_b_kernel(tc, x, adj, fc1_w, fc1_b, conv_w, base, offs, out):
 
         h0_tenth = [held.tile([LANES, N], F32, name=f"h0_tenth{cb}") for cb in range(C_BLOCKS)]
         pre = {}
+        flipped = {}
         h_nodes = {}
         r_bf16 = {}
         r_kept = {}
 
-        def mix_channels(t, cb):
+        def flip_one(cb, kb):
+            if kb == 0:
+                flipped[cb] = flips.tile([LANES, N], BF16, name="flipped")
+            nc.tensor.transpose(flipped[cb][:, block(kb)], pre[cb][:, block(kb)], identity[:])
+
+        def mix_channels(t, cb, flip_cb):
             pre[cb] = work.tile([LANES, N], BF16, name="pre")
             for hf in range(HALVES):
                 product = banks.tile([LANES, BANK], F32, name="product", tag="bank")
@@ -116,6 +122,8 @@ def tile_gcnii_b_kernel(tc, x, adj, fc1_w, fc1_b, conv_w, base, offs, out):
                     else:
                         weights, moving = conv_w_sb[:, t - 1, ib, block(cb)], r_bf16[t - 1, ib][:, half(hf)]
                     nc.tensor.matmul(product[:], weights, moving, start=(ib == 0), stop=(ib == C_BLOCKS - 1))
+                    if flip_cb is not None:
+                        flip_one(flip_cb, hf * C_BLOCKS + ib)
                 if t == 0:
                     nc.scalar.activation(pre[cb][:, half(hf)], product[:], ACT.Identity, bias=bias[:, cb : cb + 1])
                     nc.scalar.activation(
@@ -126,14 +134,11 @@ def tile_gcnii_b_kernel(tc, x, adj, fc1_w, fc1_b, conv_w, base, offs, out):
                         pre[cb][:, half(hf)], product[:], beta(t - 1), r_kept[t - 1, cb][:, half(hf)], ALU.mult, ALU.add
                     )
 
-        def flip(cb):
-            flipped = flips.tile([LANES, N], BF16, name="flipped")
-            for kb in range(N_BLOCKS):
-                nc.tensor.transpose(flipped[:, block(kb)], pre[cb][:, block(kb)], identity[:])
+        def keep_flipped(cb):
             h_nodes[cb] = work.tile([LANES, N], BF16, name="h_nodes")
-            nc.scalar.activation(h_nodes[cb][:], flipped[:], ACT.Relu)
+            nc.scalar.activation(h_nodes[cb][:], flipped[cb][:], ACT.Relu)
 
-        def propagate(t, cb):
+        def propagate(t, cb, flip_cb):
             if t < LAYERS:
                 r = work.tile([LANES, N], F32, name="r")
                 r_bf16[t, cb] = layer.tile([LANES, N], BF16, name=f"r_bf16_{cb}")
@@ -150,6 +155,8 @@ def tile_gcnii_b_kernel(tc, x, adj, fc1_w, fc1_b, conv_w, base, offs, out):
                         start=(kb == 0),
                         stop=(kb == N_BLOCKS - 1),
                     )
+                    if flip_cb is not None and hf == 0:
+                        flip_one(flip_cb, kb)
                 if t < LAYERS:
                     nc.vector.scalar_tensor_tensor(
                         r[:, half(hf)], spread[:], 1.0 - ALPHA, h0_tenth[cb][:, half(hf)], ALU.mult, ALU.add
@@ -165,8 +172,8 @@ def tile_gcnii_b_kernel(tc, x, adj, fc1_w, fc1_b, conv_w, base, offs, out):
         for t in range(LAYERS + 1):
             for step in range(C_BLOCKS + 2):
                 if step < C_BLOCKS:
-                    mix_channels(t, step)
-                if 1 <= step <= C_BLOCKS:
-                    flip(step - 1)
+                    mix_channels(t, step, step - 1 if step >= 1 else None)
                 if 2 <= step:
-                    propagate(t, step - 2)
+                    propagate(t, step - 2, step - 1 if step == C_BLOCKS else None)
+                if 1 <= step <= C_BLOCKS:
+                    keep_flipped(step - 1)

@@ -14,6 +14,7 @@ ALPHA, LAMDA = 0.1, 0.5
 BANK = 512
 C_BLOCKS, N_BLOCKS = C // LANES, N // LANES
 HALVES = N // BANK
+WAIT = 4
 assert F == C
 
 FLOPS = 2 * N * (F * C + LAYERS * C * C + (LAYERS + 1) * C * N)
@@ -21,6 +22,9 @@ FLOPS = 2 * N * (F * C + LAYERS * C * C + (LAYERS + 1) * C * N)
 
 def beta(t):
     return math.log(LAMDA / (t + 1) + 1.0)
+
+
+KEPT = 1.0 - beta(0)
 
 
 def block(b):
@@ -38,23 +42,26 @@ def tile_gcnii_b_kernel(tc, x, adj, fc1_w, fc1_b, conv_w, base, offs, out):
         tc.tile_pool(name="held", bufs=1) as held,
         tc.tile_pool(name="layer", bufs=2) as layer,
         tc.tile_pool(name="work", bufs=3) as work,
+        tc.tile_pool(name="states", bufs=4) as states,
         tc.psum_pool(name="banks", bufs=6) as banks,
         tc.psum_pool(name="flips", bufs=2) as flips,
     ):
-        offsets = lists.tile([LANES, N // 16], U16, name="offsets")
-        nc.sync.dma_start(offsets[:], offs)
-
+        fc1_w_sb = held.tile([LANES, C_BLOCKS, C], BF16, name="fc1_w_sb")
+        x_sb = held.tile([LANES, C_BLOCKS, N], BF16, name="x_sb")
+        fc1_w_rows = fc1_w.rearrange("(p ib) c -> p ib c", p=LANES)
+        x_rows = x.rearrange("(p ib) i -> p ib i", p=LANES)
+        for ibs in (slice(0, 1), slice(1, C_BLOCKS)):
+            nc.sync.dma_start(fc1_w_sb[:, ibs, :], fc1_w_rows[:, ibs, :])
+            nc.sync.dma_start(x_sb[:, ibs, :], x_rows[:, ibs, :])
         adj_sb = held.tile([LANES, N_BLOCKS, N], BF16, name="adj_sb")
         for kb in range(N_BLOCKS):
             nc.sync.dma_start(adj_sb[:, kb, :], adj[block(kb), :])
-        fc1_w_sb = held.tile([LANES, C_BLOCKS, C], BF16, name="fc1_w_sb")
-        nc.sync.dma_start(fc1_w_sb[:], fc1_w.rearrange("(ib p) c -> p ib c", p=LANES))
-        x_sb = held.tile([LANES, C_BLOCKS, N], BF16, name="x_sb")
-        for hf in range(HALVES):
-            nc.sync.dma_start(x_sb[:, :, half(hf)], x[:, half(hf)].rearrange("(ib p) i -> p ib i", p=LANES))
         conv_w_sb = held.tile([LANES, LAYERS, C_BLOCKS, C], BF16, name="conv_w_sb")
         for t in range(LAYERS):
-            nc.sync.dma_start(conv_w_sb[:, t], conv_w[t].rearrange("(ib p) d -> p ib d", p=LANES))
+            for ib in range(C_BLOCKS):
+                nc.sync.dma_start(conv_w_sb[:, t, ib, :], conv_w[t, block(ib), :])
+        offsets = lists.tile([LANES, N // 16], U16, name="offsets")
+        nc.sync.dma_start(offsets[:], offs)
         windows = [held.tile([LANES, S], F32, name=f"window{cb}") for cb in range(C_BLOCKS)]
         for cb in range(C_BLOCKS):
             nc.sync.dma_start(windows[cb][:], base[block(cb), :])
@@ -62,118 +69,221 @@ def tile_gcnii_b_kernel(tc, x, adj, fc1_w, fc1_b, conv_w, base, offs, out):
         with nc.allow_non_contiguous_dma(reason="512 bias values, one to a partition"):
             nc.gpsimd.dma_start(bias[:], fc1_b.rearrange("(cb p) one -> p (cb one)", p=LANES))
 
+        bias_kept = held.tile([LANES, C_BLOCKS], F32, name="bias_kept")
+        nc.vector.tensor_scalar_mul(bias_kept[:], bias[:], ALPHA * KEPT)
         identity = held.tile([LANES, LANES], BF16, name="identity")
         make_identity(nc, identity[:])
-        ones = held.tile([LANES, LANES], BF16, name="ones")
-        nc.vector.memset(ones[:], 1.0)
-        bias_tenth = held.tile([LANES, C_BLOCKS], F32, name="bias_tenth")
-        nc.gpsimd.tensor_scalar_mul(bias_tenth[:], bias[:], ALPHA)
+        identity_f32 = held.tile([LANES, LANES], F32, name="identity_f32")
+        make_identity(nc, identity_f32[:])
+        one = held.tile([LANES, 1], F32, name="one")
+        nc.vector.memset(one[:], 1.0)
+        nc.scalar.activation(one[:], one[:], ACT.Abs_reciprocal_sqrt)
 
-        column_sums = [banks.tile([LANES, BANK], F32, name=f"column_sums{hf}", tag="bank") for hf in range(HALVES)]
-        row_sums = held.tile([LANES, N_BLOCKS], F32, name="row_sums")
-        for kb in range(N_BLOCKS):
-            for hf in range(HALVES):
-                nc.tensor.matmul(
-                    column_sums[hf][:], ones[:], adj_sb[:, kb, half(hf)], start=(kb == 0), stop=(kb == N_BLOCKS - 1)
-                )
-            unused = work.tile([LANES, N], BF16, name="unused")
-            nc.vector.tensor_scalar(
-                unused[:], adj_sb[:, kb, :], 1.0, None, ALU.mult, ALU.add, accum_out=row_sums[:, kb : kb + 1]
-            )
-            nc.gpsimd.tensor_tensor(adj_sb[:, kb, block(kb)], adj_sb[:, kb, block(kb)], identity[:], ALU.add)
-
-        dinv_free = held.tile([LANES, N], F32, name="dinv_free")
-        for hf in range(HALVES):
-            nc.scalar.activation(dinv_free[:, half(hf)], column_sums[hf][:], ACT.Abs_reciprocal_sqrt, bias=1.0)
-        dinv_lane = held.tile([LANES, N_BLOCKS], F32, name="dinv_lane")
-        nc.scalar.activation(dinv_lane[:], row_sums[:], ACT.Abs_reciprocal_sqrt, bias=1.0)
-
-        p_sb = held.tile([LANES, N_BLOCKS, N], BF16, name="p_sb")
-        for hf in range(HALVES):
-            for kb in range(N_BLOCKS):
-                nc.vector.scalar_tensor_tensor(
-                    p_sb[:, kb, half(hf)],
-                    adj_sb[:, kb, half(hf)],
-                    dinv_lane[:, kb : kb + 1],
-                    dinv_free[:, half(hf)],
-                    ALU.mult,
-                    ALU.mult,
-                )
-
-        h0_tenth = [held.tile([LANES, N], F32, name=f"h0_tenth{cb}") for cb in range(C_BLOCKS)]
-        pre = {}
+        h0 = [held.tile([LANES, N], F32, name=f"h0_{cb}") for cb in range(C_BLOCKS)]
+        pre = [held.tile([LANES, N], BF16, name=f"h0_bf16_{cb}") for cb in range(C_BLOCKS)]
         flipped = {}
         h_nodes = {}
-        r_bf16 = {}
-        r_kept = {}
 
         def flip_one(cb, kb):
             if kb == 0:
                 flipped[cb] = flips.tile([LANES, N], BF16, name="flipped")
             nc.tensor.transpose(flipped[cb][:, block(kb)], pre[cb][:, block(kb)], identity[:])
 
-        def mix_channels(t, cb, flip_cb):
-            pre[cb] = work.tile([LANES, N], BF16, name="pre")
+        def keep_flipped(cb, pieces=1):
+            h_nodes[cb] = states.tile([LANES, N], BF16, name="h_nodes")
+            width = N // pieces
+            for piece in range(pieces):
+                cut = slice(piece * width, (piece + 1) * width)
+                nc.scalar.activation(h_nodes[cb][:, cut], flipped[cb][:, cut], ACT.Relu)
+
+        def keep_h0(cb, hf, product):
+            nc.scalar.activation(
+                h0[cb][:, half(hf)], product[:], ACT.Relu, bias=bias_kept[:, cb : cb + 1], scale=ALPHA * KEPT
+            )
+            nc.vector.tensor_scalar_mul(pre[cb][:, half(hf)], h0[cb][:, half(hf)], 1.0 / (ALPHA * KEPT))
+
+        products = [banks.tile([LANES, BANK], F32, name=f"product{cb}", tag="bank") for cb in range(C_BLOCKS)]
+        for ib in range(C_BLOCKS):
+            for cb in range(C_BLOCKS):
+                nc.tensor.matmul(
+                    products[cb][:],
+                    fc1_w_sb[:, ib, block(cb)],
+                    x_sb[:, ib, half(0)],
+                    start=(ib == 0),
+                    stop=(ib == C_BLOCKS - 1),
+                )
+        for cb in range(C_BLOCKS):
+            keep_h0(cb, 0, products[cb])
+        for cb in range(C_BLOCKS):
+            product = banks.tile([LANES, BANK], F32, name="product", tag="bank")
+            for ib in range(C_BLOCKS):
+                nc.tensor.matmul(
+                    product[:],
+                    fc1_w_sb[:, ib, block(cb)],
+                    x_sb[:, ib, half(1)],
+                    start=(ib == 0),
+                    stop=(ib == C_BLOCKS - 1),
+                )
+                if cb >= 2:
+                    flip_one(cb - 2, 2 * ib)
+                    flip_one(cb - 2, 2 * ib + 1)
+            keep_h0(cb, 1, product)
+            if cb >= 2:
+                keep_flipped(cb - 2)
+
+        row_sums = held.tile([LANES, N_BLOCKS], F32, name="row_sums")
+        dinv_lane = held.tile([LANES, N_BLOCKS], F32, name="dinv_lane")
+        rows_sb = held.tile([LANES, N_BLOCKS, N], BF16, name="rows_sb")
+        for kb in range(N_BLOCKS):
+            nc.vector.tensor_scalar(
+                rows_sb[:, kb, :], adj_sb[:, kb, :], 1.0, None, ALU.mult, ALU.add, accum_out=row_sums[:, kb : kb + 1]
+            )
+            nc.gpsimd.tensor_tensor(adj_sb[:, kb, block(kb)], adj_sb[:, kb, block(kb)], identity[:], ALU.add)
+            nc.scalar.activation(
+                dinv_lane[:, kb : kb + 1], row_sums[:, kb : kb + 1], ACT.Abs_reciprocal_sqrt, bias=1.0
+            )
+            nc.vector.tensor_scalar_mul(rows_sb[:, kb, :], adj_sb[:, kb, :], dinv_lane[:, kb : kb + 1])
+        sums_high = held.tile([LANES, N_BLOCKS], BF16, name="sums_high")
+        nc.vector.tensor_copy(sums_high[:], row_sums[:])
+        sums_low = held.tile([LANES, N_BLOCKS], BF16, name="sums_low")
+        nc.vector.tensor_tensor(sums_low[:], row_sums[:], sums_high[:], ALU.subtract)
+        dinv_free = held.tile([LANES, N], F32, name="dinv_free")
+
+        def degrees_along_free_axis():
             for hf in range(HALVES):
-                product = banks.tile([LANES, BANK], F32, name="product", tag="bank")
-                for ib in range(C_BLOCKS):
-                    if t == 0:
-                        weights, moving = fc1_w_sb[:, ib, block(cb)], x_sb[:, ib, half(hf)]
-                    else:
-                        weights, moving = conv_w_sb[:, t - 1, ib, block(cb)], r_bf16[t - 1, ib][:, half(hf)]
-                    nc.tensor.matmul(product[:], weights, moving, start=(ib == 0), stop=(ib == C_BLOCKS - 1))
-                    if flip_cb is not None:
-                        flip_one(flip_cb, hf * C_BLOCKS + ib)
-                if t == 0:
-                    nc.scalar.activation(pre[cb][:, half(hf)], product[:], ACT.Identity, bias=bias[:, cb : cb + 1])
-                    nc.scalar.activation(
-                        h0_tenth[cb][:, half(hf)], product[:], ACT.Relu, bias=bias_tenth[:, cb : cb + 1], scale=ALPHA
-                    )
-                else:
-                    nc.vector.scalar_tensor_tensor(
-                        pre[cb][:, half(hf)], product[:], beta(t - 1), r_kept[t - 1, cb][:, half(hf)], ALU.mult, ALU.add
-                    )
+                column_sums = banks.tile([LANES, BANK], F32, name="column_sums", tag="bank")
+                for q in range(BANK // LANES):
+                    kb = hf * (BANK // LANES) + q
+                    for part in (sums_high, sums_low):
+                        nc.tensor.matmul(
+                            column_sums[:, block(q)],
+                            part[:, kb : kb + 1].to_broadcast([LANES, LANES]),
+                            identity[:],
+                            start=(part is sums_high),
+                            stop=(part is sums_low),
+                        )
+                nc.scalar.activation(dinv_free[:, half(hf)], column_sums[:], ACT.Abs_reciprocal_sqrt, bias=1.0)
 
-        def keep_flipped(cb):
-            h_nodes[cb] = work.tile([LANES, N], BF16, name="h_nodes")
-            nc.scalar.activation(h_nodes[cb][:], flipped[cb][:], ACT.Relu)
+        r_bf16 = {}
+        r_kept = {}
+        p_sb = held.tile([LANES, N_BLOCKS, N], BF16, name="p_sb")
 
-        def propagate(t, cb, flip_cb):
+        def carry_flips(n, cbs, wait=WAIT):
+            first = 2 * (n - wait)
+            for j in (first, first + 1):
+                if 0 <= j < len(cbs) * N_BLOCKS:
+                    flip_one(cbs[j // N_BLOCKS], j % N_BLOCKS)
+
+        def on_tensor(t, cb):
+            return t == LAYERS - 1 and cb == C_BLOCKS - 1
+
+        def mix_channels(t, cbs, flip_cbs, wait=WAIT):
+            products = {}
+            for cb in cbs:
+                pre[cb] = work.tile([LANES, N], BF16, name="pre")
+                for hf in range(HALVES):
+                    products[cb, hf] = banks.tile([LANES, BANK], F32, name="product", tag="bank")
+            n = 0
+            for ib in range(C_BLOCKS):
+                for cb, hf in products:
+                    nc.tensor.matmul(
+                        products[cb, hf][:],
+                        conv_w_sb[:, t - 1, ib, block(cb)],
+                        r_bf16[t - 1, ib][:, half(hf)],
+                        start=(ib == 0),
+                        stop=(ib == C_BLOCKS - 1 and not on_tensor(t - 1, cb)),
+                    )
+                    carry_flips(n, flip_cbs, wait)
+                    n += 1
+            for cb, hf in products:
+                if on_tensor(t - 1, cb):
+                    nc.tensor.matmul(
+                        products[cb, hf][:], identity_f32[:], r_kept[t - 1, cb][:, half(hf)], start=False, stop=True
+                    )
+                    nc.scalar.mul(pre[cb][:, half(hf)], products[cb, hf][:], beta(t - 1))
+                    continue
+                nc.vector.scalar_tensor_tensor(
+                    pre[cb][:, half(hf)],
+                    products[cb, hf][:],
+                    beta(t - 1),
+                    r_kept[t - 1, cb][:, half(hf)],
+                    ALU.mult,
+                    ALU.add,
+                )
+
+        def propagate(t, cb, flip_cbs, between=None):
             if t < LAYERS:
-                r = work.tile([LANES, N], F32, name="r")
                 r_bf16[t, cb] = layer.tile([LANES, N], BF16, name=f"r_bf16_{cb}")
                 r_kept[t, cb] = layer.tile([LANES, N], F32, name=f"r_kept_{cb}")
+                r = r_kept[t, cb] if t == 0 else work.tile([LANES, N], F32, name="r")
             else:
-                term = work.tile([LANES, N], F32, name="term")
+                term = work.tile([LANES, N], F32, name="term", tag="r")
+            moving = rows_sb if t == 0 else p_sb
             for hf in range(HALVES):
                 spread = banks.tile([LANES, BANK], F32, name="spread", tag="bank")
                 for kb in range(N_BLOCKS):
                     nc.tensor.matmul(
                         spread[:],
                         h_nodes[cb][:, block(kb)],
-                        p_sb[:, kb, half(hf)],
+                        moving[:, kb, half(hf)],
                         start=(kb == 0),
                         stop=(kb == N_BLOCKS - 1),
                     )
-                    if flip_cb is not None and hf == 0:
-                        flip_one(flip_cb, kb)
+                    carry_flips(hf * N_BLOCKS + kb, flip_cbs)
+                if between is not None and hf == 0:
+                    between()
                 if t < LAYERS:
-                    nc.vector.scalar_tensor_tensor(
-                        r[:, half(hf)], spread[:], 1.0 - ALPHA, h0_tenth[cb][:, half(hf)], ALU.mult, ALU.add
-                    )
-                    nc.scalar.copy(r_bf16[t, cb][:, half(hf)], r[:, half(hf)])
-                    nc.scalar.mul(r_kept[t, cb][:, half(hf)], r[:, half(hf)], 1.0 - beta(t))
+                    if t == 0:
+                        scaled = work.tile([LANES, BANK], F32, name="scaled")
+                        nc.vector.scalar_tensor_tensor(
+                            scaled[:], spread[:], (1.0 - ALPHA) * KEPT, dinv_free[:, half(hf)], ALU.mult, ALU.mult
+                        )
+                        nc.vector.tensor_tensor(r[:, half(hf)], scaled[:], h0[cb][:, half(hf)], ALU.add)
+                    else:
+                        nc.vector.scalar_tensor_tensor(
+                            r[:, half(hf)], spread[:], (1.0 - ALPHA) * KEPT, h0[cb][:, half(hf)], ALU.mult, ALU.add
+                        )
+                    nc.scalar.mul(r_bf16[t, cb][:, half(hf)], r[:, half(hf)], 1.0 / KEPT)
+                    if t > 0:
+                        nc.scalar.mul(r_kept[t, cb][:, half(hf)], r[:, half(hf)], (1.0 - beta(t)) / KEPT / (beta(t) if on_tensor(t, cb) else 1.0))
                 else:
                     nc.scalar.mul(term[:, half(hf)], spread[:], 1.0 - ALPHA)
+            if t == LAYERS - 1:
+                nc.scalar.mul(h0[cb][:], h0[cb][:], 1.0 / KEPT)
             if t == LAYERS:
-                nc.vector.tensor_tensor(windows[cb][:].indirect(offsets[:]), term[:], h0_tenth[cb][:], ALU.add)
+                nc.vector.tensor_tensor(windows[cb][:].indirect(offsets[:]), term[:], h0[cb][:], ALU.add)
                 nc.sync.dma_start(out[block(cb), :], windows[cb][:])
 
-        for t in range(LAYERS + 1):
-            for step in range(C_BLOCKS + 2):
-                if step < C_BLOCKS:
-                    mix_channels(t, step, step - 1 if step >= 1 else None)
-                if 2 <= step:
-                    propagate(t, step - 2, step - 1 if step == C_BLOCKS else None)
-                if 1 <= step <= C_BLOCKS:
-                    keep_flipped(step - 1)
+        propagate(0, 0, (2, 3), degrees_along_free_axis)
+        keep_flipped(2)
+        keep_flipped(3)
+        for cb in range(1, C_BLOCKS):
+            propagate(0, cb, ())
+
+        for kb in range(N_BLOCKS):
+            full = work.tile([LANES, N], BF16, name="full")
+            nc.scalar.mul(full[:], dinv_free[:], dinv_lane[:, kb : kb + 1])
+            nc.gpsimd.tensor_tensor(p_sb[:, kb, :], full[:], adj_sb[:, kb, :], ALU.mult)
+
+        for t in range(1, LAYERS):
+            mix_channels(t, (0, 1), ())
+            mix_channels(t, (2, 3), (0, 1))
+            keep_flipped(0)
+            keep_flipped(1)
+            propagate(t, 0, (2, 3))
+            keep_flipped(2)
+            keep_flipped(3)
+            for cb in range(1, C_BLOCKS):
+                propagate(t, cb, ())
+        t = LAYERS
+        mix_channels(t, (0, 1), ())
+        mix_channels(t, (2,), (0,), 2)
+        keep_flipped(0, 2)
+        propagate(t, 0, (1, 2))
+        keep_flipped(1)
+        keep_flipped(2)
+        propagate(t, 1, ())
+        mix_channels(t, (3,), ())
+        propagate(t, 2, (3,))
+        keep_flipped(3)
+        propagate(t, 3, ())

@@ -263,7 +263,7 @@ def tile_gcnii_b_kernel(tc, x, adj, fc1_w, fc1_b, conv_w, base, offs, out):
         for kb in range(N_BLOCKS):
             full = work.tile([LANES, N], BF16, name="full")
             nc.scalar.mul(full[:], dinv_free[:], dinv_lane[:, kb : kb + 1])
-            nc.gpsimd.tensor_tensor(p_sb[:, kb, :], full[:], adj_sb[:, kb, :], ALU.mult)
+            nc.vector.tensor_tensor(p_sb[:, kb, :], full[:], adj_sb[:, kb, :], ALU.mult)
 
         for t in range(1, LAYERS):
             mix_channels(t, (0, 1), ())

@@ -14,7 +14,11 @@ ALPHA, LAMDA = 0.1, 0.5
 BANK = 512
 C_BLOCKS, N_BLOCKS = C // LANES, N // LANES
 HALVES = N // BANK
+QUARTERS = BANK // LANES
 WAIT = 4
+LAST = 8
+LOW_FIRST, LOW_SECOND = ((0, 0), (1, 0)), ((0, 1), (1, 1))
+HIGH_FIRST, HIGH_SECOND = ((2, 0), (3, 0)), ((2, 1), (3, 1))
 assert F == C
 
 FLOPS = 2 * N * (F * C + LAYERS * C * C + (LAYERS + 1) * C * N)
@@ -42,7 +46,8 @@ def tile_gcnii_b_kernel(tc, x, adj, fc1_w, fc1_b, conv_w, base, offs, out):
         tc.tile_pool(name="held", bufs=1) as held,
         tc.tile_pool(name="layer", bufs=2) as layer,
         tc.tile_pool(name="work", bufs=3) as work,
-        tc.tile_pool(name="states", bufs=4) as states,
+        tc.tile_pool(name="parts", bufs=10) as parts_pool,
+        tc.tile_pool(name="states", bufs=5) as states,
         tc.psum_pool(name="banks", bufs=6) as banks,
         tc.psum_pool(name="flips", bufs=2) as flips,
     ):
@@ -73,63 +78,68 @@ def tile_gcnii_b_kernel(tc, x, adj, fc1_w, fc1_b, conv_w, base, offs, out):
         nc.vector.tensor_scalar_mul(bias_kept[:], bias[:], ALPHA * KEPT)
         identity = held.tile([LANES, LANES], BF16, name="identity")
         make_identity(nc, identity[:])
-        identity_f32 = held.tile([LANES, LANES], F32, name="identity_f32")
-        make_identity(nc, identity_f32[:])
         one = held.tile([LANES, 1], F32, name="one")
         nc.vector.memset(one[:], 1.0)
         nc.scalar.activation(one[:], one[:], ACT.Abs_reciprocal_sqrt)
 
         h0 = [held.tile([LANES, N], F32, name=f"h0_{cb}") for cb in range(C_BLOCKS)]
-        pre = [held.tile([LANES, N], BF16, name=f"h0_bf16_{cb}") for cb in range(C_BLOCKS)]
-        flipped = {}
+        pre = {}
         h_nodes = {}
+        spreads = {}
 
-        def flip_one(cb, kb):
-            if kb == 0:
-                flipped[cb] = flips.tile([LANES, N], BF16, name="flipped")
-            nc.tensor.transpose(flipped[cb][:, block(kb)], pre[cb][:, block(kb)], identity[:])
+        def run(matmuls, parts=(), wait=0):
+            flipped = flips.tile([LANES, N], BF16, name="flipped") if parts else None
+            blocks = [(j, part, q) for j, part in enumerate(parts) for q in range(QUARTERS)]
+            done = 0
+            for n, (product, stationary, moving, start, stop) in enumerate(matmuls):
+                nc.tensor.matmul(product, stationary, moving, start=start, stop=stop)
+                due = len(blocks) if n == len(matmuls) - 1 else max(0, 2 * (n + 1 - wait))
+                for j, part, q in blocks[done:due]:
+                    nc.tensor.transpose(flipped[:, block(j * QUARTERS + q)], pre[part][:, block(q)], identity[:])
+                done = max(done, min(due, len(blocks)))
+            return flipped
 
-        def keep_flipped(cb, pieces=1):
-            h_nodes[cb] = states.tile([LANES, N], BF16, name="h_nodes")
-            width = N // pieces
+        def keep(flipped, parts, pieces=1):
+            nodes_first = states.tile([LANES, N], BF16, name="nodes_first")
+            width = len(parts) * BANK // pieces
             for piece in range(pieces):
                 cut = slice(piece * width, (piece + 1) * width)
-                nc.scalar.activation(h_nodes[cb][:, cut], flipped[cb][:, cut], ACT.Relu)
+                nc.scalar.activation(nodes_first[:, cut], flipped[:, cut], ACT.Relu)
+            for j, part in enumerate(parts):
+                h_nodes[part] = nodes_first[:, half(j)]
 
         def keep_h0(cb, hf, product):
             nc.scalar.activation(
                 h0[cb][:, half(hf)], product[:], ACT.Relu, bias=bias_kept[:, cb : cb + 1], scale=ALPHA * KEPT
             )
-            nc.vector.tensor_scalar_mul(pre[cb][:, half(hf)], h0[cb][:, half(hf)], 1.0 / (ALPHA * KEPT))
+            pre[cb, hf] = parts_pool.tile([LANES, BANK], BF16, name="pre")
+            nc.vector.tensor_scalar_mul(pre[cb, hf][:], h0[cb][:, half(hf)], 1.0 / (ALPHA * KEPT))
 
-        products = [banks.tile([LANES, BANK], F32, name=f"product{cb}", tag="bank") for cb in range(C_BLOCKS)]
-        for ib in range(C_BLOCKS):
-            for cb in range(C_BLOCKS):
-                nc.tensor.matmul(
+        for hf in range(HALVES):
+            products = [banks.tile([LANES, BANK], F32, name=f"product{cb}", tag="bank") for cb in range(C_BLOCKS)]
+            order = [(cb, ib) for ib in range(C_BLOCKS) for cb in range(C_BLOCKS)]
+            if hf == 1:
+                order = [(cb, ib) for cb in range(C_BLOCKS) for ib in range(C_BLOCKS)]
+            matmuls = [
+                (
                     products[cb][:],
                     fc1_w_sb[:, ib, block(cb)],
-                    x_sb[:, ib, half(0)],
-                    start=(ib == 0),
-                    stop=(ib == C_BLOCKS - 1),
+                    x_sb[:, ib, half(hf)],
+                    ib == 0,
+                    ib == C_BLOCKS - 1,
                 )
-        for cb in range(C_BLOCKS):
-            keep_h0(cb, 0, products[cb])
-        for cb in range(C_BLOCKS):
-            product = banks.tile([LANES, BANK], F32, name="product", tag="bank")
-            for ib in range(C_BLOCKS):
-                nc.tensor.matmul(
-                    product[:],
-                    fc1_w_sb[:, ib, block(cb)],
-                    x_sb[:, ib, half(1)],
-                    start=(ib == 0),
-                    stop=(ib == C_BLOCKS - 1),
-                )
-                if cb >= 2:
-                    flip_one(cb - 2, 2 * ib)
-                    flip_one(cb - 2, 2 * ib + 1)
-            keep_h0(cb, 1, product)
-            if cb >= 2:
-                keep_flipped(cb - 2)
+                for cb, ib in order
+            ]
+            if hf == 0:
+                run(matmuls)
+            else:
+                run(matmuls[:8])
+                low = run(matmuls[8:12], LOW_FIRST)
+                high = run(matmuls[12:], HIGH_FIRST)
+                keep(low, LOW_FIRST, 2)
+                keep(high, HIGH_FIRST)
+            for cb in range(C_BLOCKS):
+                keep_h0(cb, hf, products[cb])
 
         row_sums = held.tile([LANES, N_BLOCKS], F32, name="row_sums")
         dinv_lane = held.tile([LANES, N_BLOCKS], F32, name="dinv_lane")
@@ -152,8 +162,8 @@ def tile_gcnii_b_kernel(tc, x, adj, fc1_w, fc1_b, conv_w, base, offs, out):
         def degrees_along_free_axis():
             for hf in range(HALVES):
                 column_sums = banks.tile([LANES, BANK], F32, name="column_sums", tag="bank")
-                for q in range(BANK // LANES):
-                    kb = hf * (BANK // LANES) + q
+                for q in range(QUARTERS):
+                    kb = hf * QUARTERS + q
                     for part in (sums_high, sums_low):
                         nc.tensor.matmul(
                             column_sums[:, block(q)],
@@ -168,97 +178,96 @@ def tile_gcnii_b_kernel(tc, x, adj, fc1_w, fc1_b, conv_w, base, offs, out):
         r_kept = {}
         p_sb = held.tile([LANES, N_BLOCKS, N], BF16, name="p_sb")
 
-        def carry_flips(n, cbs, wait=WAIT):
-            first = 2 * (n - wait)
-            for j in (first, first + 1):
-                if 0 <= j < len(cbs) * N_BLOCKS:
-                    flip_one(cbs[j // N_BLOCKS], j % N_BLOCKS)
-
-        def on_tensor(t, cb):
-            return t == LAYERS - 1 and cb == C_BLOCKS - 1
-
-        def mix_channels(t, cbs, flip_cbs, wait=WAIT):
-            products = {}
-            for cb in cbs:
-                pre[cb] = work.tile([LANES, N], BF16, name="pre")
-                for hf in range(HALVES):
-                    products[cb, hf] = banks.tile([LANES, BANK], F32, name="product", tag="bank")
-            n = 0
-            for ib in range(C_BLOCKS):
-                for cb, hf in products:
-                    nc.tensor.matmul(
-                        products[cb, hf][:],
-                        conv_w_sb[:, t - 1, ib, block(cb)],
-                        r_bf16[t - 1, ib][:, half(hf)],
-                        start=(ib == 0),
-                        stop=(ib == C_BLOCKS - 1 and not on_tensor(t - 1, cb)),
-                    )
-                    carry_flips(n, flip_cbs, wait)
-                    n += 1
-            for cb, hf in products:
-                if on_tensor(t - 1, cb):
-                    nc.tensor.matmul(
-                        products[cb, hf][:], identity_f32[:], r_kept[t - 1, cb][:, half(hf)], start=False, stop=True
-                    )
-                    nc.scalar.mul(pre[cb][:, half(hf)], products[cb, hf][:], beta(t - 1))
-                    continue
+        def mix_channels(t, parts, flip_parts=(), wait=0):
+            products = {part: banks.tile([LANES, BANK], F32, name="product", tag="bank") for part in parts}
+            matmuls = []
+            for cb, hf in parts:
+                for ib in range(C_BLOCKS):
+                    stationary, moving = conv_w_sb[:, t - 1, ib, block(cb)], r_bf16[t - 1, ib][:, half(hf)]
+                    matmuls.append((products[cb, hf][:], stationary, moving, ib == 0, ib == C_BLOCKS - 1))
+            flipped = run(matmuls, flip_parts, wait)
+            for cb, hf in parts:
+                pre[cb, hf] = parts_pool.tile([LANES, BANK], BF16, name="pre")
                 nc.vector.scalar_tensor_tensor(
-                    pre[cb][:, half(hf)],
+                    pre[cb, hf][:],
                     products[cb, hf][:],
                     beta(t - 1),
                     r_kept[t - 1, cb][:, half(hf)],
                     ALU.mult,
                     ALU.add,
                 )
+            return flipped
 
-        def propagate(t, cb, flip_cbs, between=None):
-            if t < LAYERS:
-                r_bf16[t, cb] = layer.tile([LANES, N], BF16, name=f"r_bf16_{cb}")
-                r_kept[t, cb] = layer.tile([LANES, N], F32, name=f"r_kept_{cb}")
-                r = r_kept[t, cb] if t == 0 else work.tile([LANES, N], F32, name="r")
-            else:
-                term = work.tile([LANES, N], F32, name="term", tag="r")
+        def spread_nodes(t, parts, node_half, flip_parts=(), wait=0):
             moving = rows_sb if t == 0 else p_sb
-            for hf in range(HALVES):
-                spread = banks.tile([LANES, BANK], F32, name="spread", tag="bank")
-                for kb in range(N_BLOCKS):
-                    nc.tensor.matmul(
-                        spread[:],
-                        h_nodes[cb][:, block(kb)],
-                        moving[:, kb, half(hf)],
-                        start=(kb == 0),
-                        stop=(kb == N_BLOCKS - 1),
+            matmuls = []
+            for cb, hf in parts:
+                if node_half == 0:
+                    spreads[cb, hf] = banks.tile([LANES, BANK], F32, name="spread", tag="bank")
+                for q in range(QUARTERS):
+                    kb = node_half * QUARTERS + q
+                    matmuls.append(
+                        (
+                            spreads[cb, hf][:],
+                            h_nodes[cb, node_half][:, block(q)],
+                            moving[:, kb, half(hf)],
+                            kb == 0,
+                            kb == N_BLOCKS - 1,
+                        )
                     )
-                    carry_flips(hf * N_BLOCKS + kb, flip_cbs)
-                if between is not None and hf == 0:
-                    between()
-                if t < LAYERS:
-                    if t == 0:
-                        scaled = work.tile([LANES, BANK], F32, name="scaled")
-                        nc.vector.scalar_tensor_tensor(
-                            scaled[:], spread[:], (1.0 - ALPHA) * KEPT, dinv_free[:, half(hf)], ALU.mult, ALU.mult
-                        )
-                        nc.vector.tensor_tensor(r[:, half(hf)], scaled[:], h0[cb][:, half(hf)], ALU.add)
-                    else:
-                        nc.vector.scalar_tensor_tensor(
-                            r[:, half(hf)], spread[:], (1.0 - ALPHA) * KEPT, h0[cb][:, half(hf)], ALU.mult, ALU.add
-                        )
-                    nc.scalar.mul(r_bf16[t, cb][:, half(hf)], r[:, half(hf)], 1.0 / KEPT)
-                    if t > 0:
-                        nc.scalar.mul(r_kept[t, cb][:, half(hf)], r[:, half(hf)], (1.0 - beta(t)) / KEPT / (beta(t) if on_tensor(t, cb) else 1.0))
-                else:
-                    nc.scalar.mul(term[:, half(hf)], spread[:], 1.0 - ALPHA)
-            if t == LAYERS - 1:
-                nc.scalar.mul(h0[cb][:], h0[cb][:], 1.0 / KEPT)
-            if t == LAYERS:
-                nc.vector.tensor_tensor(windows[cb][:].indirect(offsets[:]), term[:], h0[cb][:], ALU.add)
-                nc.sync.dma_start(out[block(cb), :], windows[cb][:])
+            return run(matmuls, flip_parts, wait)
 
-        propagate(0, 0, (2, 3), degrees_along_free_axis)
-        keep_flipped(2)
-        keep_flipped(3)
-        for cb in range(1, C_BLOCKS):
-            propagate(0, cb, ())
+        def take_r(t, parts):
+            for cb, hf in parts:
+                if hf == 0:
+                    r_bf16[t, cb] = layer.tile([LANES, N], BF16, name=f"r_bf16_{cb}")
+                    r_kept[t, cb] = layer.tile([LANES, N], F32, name=f"r_kept_{cb}")
+                if t == 0:
+                    scaled = work.tile([LANES, BANK], F32, name="scaled")
+                    nc.vector.scalar_tensor_tensor(
+                        scaled[:],
+                        spreads[cb, hf][:],
+                        (1.0 - ALPHA) * KEPT,
+                        dinv_free[:, half(hf)],
+                        ALU.mult,
+                        ALU.mult,
+                    )
+                    r = r_kept[t, cb][:, half(hf)]
+                    nc.vector.tensor_tensor(r, scaled[:], h0[cb][:, half(hf)], ALU.add)
+                    nc.scalar.mul(r_bf16[t, cb][:, half(hf)], r, 1.0 / KEPT)
+                else:
+                    r = work.tile([LANES, BANK], F32, name="r")
+                    nc.vector.scalar_tensor_tensor(
+                        r[:], spreads[cb, hf][:], (1.0 - ALPHA) * KEPT, h0[cb][:, half(hf)], ALU.mult, ALU.add
+                    )
+                    nc.scalar.mul(r_bf16[t, cb][:, half(hf)], r[:], 1.0 / KEPT)
+                    nc.scalar.mul(r_kept[t, cb][:, half(hf)], r[:], (1.0 - beta(t)) / KEPT)
+
+        def make_h0_term(cb):
+            nc.vector.tensor_scalar_mul(h0[cb][:], h0[cb][:], 1.0 / KEPT)
+
+        def scatter(cb):
+            term = work.tile([LANES, N], F32, name="term")
+            for hf in range(HALVES):
+                nc.scalar.mul(term[:, half(hf)], spreads[cb, hf][:], 1.0 - ALPHA)
+            nc.vector.tensor_tensor(windows[cb][:].indirect(offsets[:]), term[:], h0[cb][:], ALU.add)
+            nc.sync.dma_start(out[block(cb), :], windows[cb][:])
+
+        all_blocks = range(C_BLOCKS)
+
+        def at_half(hf):
+            return [(cb, hf) for cb in all_blocks]
+
+        low = spread_nodes(0, at_half(0)[:2], 0, LOW_SECOND, WAIT)
+        high = spread_nodes(0, at_half(0)[2:], 0, HIGH_SECOND, WAIT)
+        keep(low, LOW_SECOND)
+        keep(high, HIGH_SECOND)
+        degrees_along_free_axis()
+        spread_nodes(0, at_half(0), 1)
+        take_r(0, at_half(0))
+        spread_nodes(0, at_half(1), 0)
+        spread_nodes(0, at_half(1), 1)
+        take_r(0, at_half(1))
 
         for kb in range(N_BLOCKS):
             full = work.tile([LANES, N], BF16, name="full")
@@ -266,24 +275,44 @@ def tile_gcnii_b_kernel(tc, x, adj, fc1_w, fc1_b, conv_w, base, offs, out):
             nc.vector.tensor_tensor(p_sb[:, kb, :], full[:], adj_sb[:, kb, :], ALU.mult)
 
         for t in range(1, LAYERS):
-            mix_channels(t, (0, 1), ())
-            mix_channels(t, (2, 3), (0, 1))
-            keep_flipped(0)
-            keep_flipped(1)
-            propagate(t, 0, (2, 3))
-            keep_flipped(2)
-            keep_flipped(3)
-            for cb in range(1, C_BLOCKS):
-                propagate(t, cb, ())
+            mix_channels(t, at_half(0))
+            low = mix_channels(t, at_half(1)[:2], LOW_FIRST, WAIT)
+            high = mix_channels(t, at_half(1)[2:], HIGH_FIRST, WAIT)
+            keep(low, LOW_FIRST)
+            keep(high, HIGH_FIRST)
+            low = spread_nodes(t, at_half(0)[:2], 0, LOW_SECOND, WAIT)
+            high = spread_nodes(t, at_half(0)[2:], 0, HIGH_SECOND, WAIT)
+            keep(low, LOW_SECOND)
+            keep(high, HIGH_SECOND)
+            spread_nodes(t, at_half(0), 1)
+            take_r(t, at_half(0))
+            spread_nodes(t, at_half(1), 0)
+            spread_nodes(t, at_half(1), 1)
+            take_r(t, at_half(1))
+
         t = LAYERS
-        mix_channels(t, (0, 1), ())
-        mix_channels(t, (2,), (0,), 2)
-        keep_flipped(0, 2)
-        propagate(t, 0, (1, 2))
-        keep_flipped(1)
-        keep_flipped(2)
-        propagate(t, 1, ())
-        mix_channels(t, (3,), ())
-        propagate(t, 2, (3,))
-        keep_flipped(3)
-        propagate(t, 3, ())
+        make_h0_term(0)
+        mix_channels(t, [(0, 0), (1, 0)])
+        flipped = mix_channels(t, [(0, 1), (1, 1)], [(0, 0)], WAIT)
+        keep(flipped, [(0, 0)])
+        flipped = spread_nodes(t, [(0, 0), (0, 1)], 0, [(0, 1)], WAIT)
+        keep(flipped, [(0, 1)])
+        flipped = spread_nodes(t, [(0, 0), (0, 1)], 1, [(1, 0), (1, 1)])
+        keep(flipped, [(1, 0), (1, 1)])
+        scatter(0)
+        make_h0_term(1)
+        mix_channels(t, [(2, 0), (2, 1)])
+        mix_channels(t, [(3, 0), (3, 1)])
+        spread_nodes(t, [(1, 0), (1, 1)], 0)
+        flipped = spread_nodes(t, [(1, 0), (1, 1)], 1, [(2, 0), (2, 1)], LAST)
+        keep(flipped, [(2, 0), (2, 1)])
+        scatter(1)
+        make_h0_term(2)
+        flipped = spread_nodes(t, [(2, 0), (2, 1)], 0, [(3, 0), (3, 1)], WAIT)
+        keep(flipped, [(3, 0), (3, 1)])
+        spread_nodes(t, [(2, 0), (2, 1)], 1)
+        scatter(2)
+        make_h0_term(3)
+        for node_half in range(HALVES):
+            spread_nodes(t, [(3, 0), (3, 1)], node_half)
+        scatter(3)

@@ -15,8 +15,6 @@ BANK = 512
 C_BLOCKS, N_BLOCKS = C // LANES, N // LANES
 HALVES = N // BANK
 QUARTERS = BANK // LANES
-WAIT = 4
-LAST = 8
 LOW_FIRST, LOW_SECOND = ((0, 0), (1, 0)), ((0, 1), (1, 1))
 HIGH_FIRST, HIGH_SECOND = ((2, 0), (3, 0)), ((2, 1), (3, 1))
 assert F == C
@@ -44,6 +42,7 @@ def tile_gcnii_b_kernel(tc, x, adj, fc1_w, fc1_b, conv_w, base, offs, out):
     with (
         tc.tile_pool(name="lists", bufs=1) as lists,
         tc.tile_pool(name="held", bufs=1) as held,
+        tc.tile_pool(name="reused", bufs=1) as reused,
         tc.tile_pool(name="layer", bufs=2) as layer,
         tc.tile_pool(name="work", bufs=3) as work,
         tc.tile_pool(name="parts", bufs=10) as parts_pool,
@@ -78,6 +77,8 @@ def tile_gcnii_b_kernel(tc, x, adj, fc1_w, fc1_b, conv_w, base, offs, out):
         nc.vector.tensor_scalar_mul(bias_kept[:], bias[:], ALPHA * KEPT)
         identity = held.tile([LANES, LANES], BF16, name="identity")
         make_identity(nc, identity[:])
+        identity_f32 = held.tile([LANES, LANES], F32, name="identity_f32")
+        make_identity(nc, identity_f32[:])
         one = held.tile([LANES, 1], F32, name="one")
         nc.vector.memset(one[:], 1.0)
         nc.scalar.activation(one[:], one[:], ACT.Abs_reciprocal_sqrt)
@@ -87,16 +88,14 @@ def tile_gcnii_b_kernel(tc, x, adj, fc1_w, fc1_b, conv_w, base, offs, out):
         h_nodes = {}
         spreads = {}
 
-        def run(matmuls, parts=(), wait=0):
+        def run(matmuls, parts=(), each=1):
             flipped = flips.tile([LANES, N], BF16, name="flipped") if parts else None
             blocks = [(j, part, q) for j, part in enumerate(parts) for q in range(QUARTERS)]
-            done = 0
             for n, (product, stationary, moving, start, stop) in enumerate(matmuls):
                 nc.tensor.matmul(product, stationary, moving, start=start, stop=stop)
-                due = len(blocks) if n == len(matmuls) - 1 else max(0, 2 * (n + 1 - wait))
-                for j, part, q in blocks[done:due]:
+                due = each * n + each if n < len(matmuls) - 1 else len(blocks)
+                for j, part, q in blocks[each * n : due]:
                     nc.tensor.transpose(flipped[:, block(j * QUARTERS + q)], pre[part][:, block(q)], identity[:])
-                done = max(done, min(due, len(blocks)))
             return flipped
 
         def keep(flipped, parts, pieces=1):
@@ -134,8 +133,8 @@ def tile_gcnii_b_kernel(tc, x, adj, fc1_w, fc1_b, conv_w, base, offs, out):
                 run(matmuls)
             else:
                 run(matmuls[:8])
-                low = run(matmuls[8:12], LOW_FIRST)
-                high = run(matmuls[12:], HIGH_FIRST)
+                low = run(matmuls[8:12], LOW_FIRST, 2)
+                high = run(matmuls[12:], HIGH_FIRST, 2)
                 keep(low, LOW_FIRST, 2)
                 keep(high, HIGH_FIRST)
             for cb in range(C_BLOCKS):
@@ -143,12 +142,12 @@ def tile_gcnii_b_kernel(tc, x, adj, fc1_w, fc1_b, conv_w, base, offs, out):
 
         row_sums = held.tile([LANES, N_BLOCKS], F32, name="row_sums")
         dinv_lane = held.tile([LANES, N_BLOCKS], F32, name="dinv_lane")
-        rows_sb = held.tile([LANES, N_BLOCKS, N], BF16, name="rows_sb")
+        rows_sb = reused.tile([LANES, N_BLOCKS, N], BF16, name="rows_sb", tag="rows")
         for kb in range(N_BLOCKS):
             nc.vector.tensor_scalar(
                 rows_sb[:, kb, :], adj_sb[:, kb, :], 1.0, None, ALU.mult, ALU.add, accum_out=row_sums[:, kb : kb + 1]
             )
-            nc.gpsimd.tensor_tensor(adj_sb[:, kb, block(kb)], adj_sb[:, kb, block(kb)], identity[:], ALU.add)
+            nc.vector.tensor_tensor(adj_sb[:, kb, block(kb)], adj_sb[:, kb, block(kb)], identity[:], ALU.add)
             nc.scalar.activation(
                 dinv_lane[:, kb : kb + 1], row_sums[:, kb : kb + 1], ACT.Abs_reciprocal_sqrt, bias=1.0
             )
@@ -178,16 +177,25 @@ def tile_gcnii_b_kernel(tc, x, adj, fc1_w, fc1_b, conv_w, base, offs, out):
         r_kept = {}
         p_sb = held.tile([LANES, N_BLOCKS, N], BF16, name="p_sb")
 
-        def mix_channels(t, parts, flip_parts=(), wait=0):
+        def on_tensor(t, cb):
+            return t == LAYERS - 1 and cb == C_BLOCKS - 1
+
+        def mix_channels(t, parts, flip_parts=(), each=1):
             products = {part: banks.tile([LANES, BANK], F32, name="product", tag="bank") for part in parts}
             matmuls = []
             for cb, hf in parts:
                 for ib in range(C_BLOCKS):
                     stationary, moving = conv_w_sb[:, t - 1, ib, block(cb)], r_bf16[t - 1, ib][:, half(hf)]
-                    matmuls.append((products[cb, hf][:], stationary, moving, ib == 0, ib == C_BLOCKS - 1))
-            flipped = run(matmuls, flip_parts, wait)
+                    stop = ib == C_BLOCKS - 1 and not on_tensor(t - 1, cb)
+                    matmuls.append((products[cb, hf][:], stationary, moving, ib == 0, stop))
+                if on_tensor(t - 1, cb):
+                    matmuls.append((products[cb, hf][:], identity_f32[:], r_kept[t - 1, cb][:, half(hf)], False, True))
+            flipped = run(matmuls, flip_parts, each)
             for cb, hf in parts:
                 pre[cb, hf] = parts_pool.tile([LANES, BANK], BF16, name="pre")
+                if on_tensor(t - 1, cb):
+                    nc.scalar.mul(pre[cb, hf][:], products[cb, hf][:], beta(t - 1))
+                    continue
                 nc.vector.scalar_tensor_tensor(
                     pre[cb, hf][:],
                     products[cb, hf][:],
@@ -198,7 +206,7 @@ def tile_gcnii_b_kernel(tc, x, adj, fc1_w, fc1_b, conv_w, base, offs, out):
                 )
             return flipped
 
-        def spread_nodes(t, parts, node_half, flip_parts=(), wait=0):
+        def spread_nodes(t, parts, node_half, flip_parts=(), each=1):
             moving = rows_sb if t == 0 else p_sb
             matmuls = []
             for cb, hf in parts:
@@ -215,7 +223,7 @@ def tile_gcnii_b_kernel(tc, x, adj, fc1_w, fc1_b, conv_w, base, offs, out):
                             kb == N_BLOCKS - 1,
                         )
                     )
-            return run(matmuls, flip_parts, wait)
+            return run(matmuls, flip_parts, each)
 
         def take_r(t, parts):
             for cb, hf in parts:
@@ -241,25 +249,29 @@ def tile_gcnii_b_kernel(tc, x, adj, fc1_w, fc1_b, conv_w, base, offs, out):
                         r[:], spreads[cb, hf][:], (1.0 - ALPHA) * KEPT, h0[cb][:, half(hf)], ALU.mult, ALU.add
                     )
                     nc.scalar.mul(r_bf16[t, cb][:, half(hf)], r[:], 1.0 / KEPT)
-                    nc.scalar.mul(r_kept[t, cb][:, half(hf)], r[:], (1.0 - beta(t)) / KEPT)
+                    share = (1.0 - beta(t)) / KEPT / (beta(t) if on_tensor(t, cb) else 1.0)
+                    nc.scalar.mul(r_kept[t, cb][:, half(hf)], r[:], share)
 
-        def make_h0_term(cb):
-            nc.vector.tensor_scalar_mul(h0[cb][:], h0[cb][:], 1.0 / KEPT)
-
-        def scatter(cb):
+        def scatter(cb, h0_tenth):
             term = work.tile([LANES, N], F32, name="term")
             for hf in range(HALVES):
                 nc.scalar.mul(term[:, half(hf)], spreads[cb, hf][:], 1.0 - ALPHA)
-            nc.vector.tensor_tensor(windows[cb][:].indirect(offsets[:]), term[:], h0[cb][:], ALU.add)
+            nc.vector.tensor_tensor(windows[cb][:].indirect(offsets[:]), term[:], h0_tenth[:, cb, :], ALU.add)
             nc.sync.dma_start(out[block(cb), :], windows[cb][:])
+
+        def make_p():
+            for kb in range(N_BLOCKS):
+                full = work.tile([LANES, N], BF16, name="full")
+                nc.scalar.mul(full[:], dinv_free[:], dinv_lane[:, kb : kb + 1])
+                nc.vector.tensor_tensor(p_sb[:, kb, :], full[:], adj_sb[:, kb, :], ALU.mult)
 
         all_blocks = range(C_BLOCKS)
 
         def at_half(hf):
             return [(cb, hf) for cb in all_blocks]
 
-        low = spread_nodes(0, at_half(0)[:2], 0, LOW_SECOND, WAIT)
-        high = spread_nodes(0, at_half(0)[2:], 0, HIGH_SECOND, WAIT)
+        low = spread_nodes(0, at_half(0)[:2], 0, LOW_SECOND)
+        high = spread_nodes(0, at_half(0)[2:], 0, HIGH_SECOND)
         keep(low, LOW_SECOND)
         keep(high, HIGH_SECOND)
         degrees_along_free_axis()
@@ -269,50 +281,48 @@ def tile_gcnii_b_kernel(tc, x, adj, fc1_w, fc1_b, conv_w, base, offs, out):
         spread_nodes(0, at_half(1), 1)
         take_r(0, at_half(1))
 
-        for kb in range(N_BLOCKS):
-            full = work.tile([LANES, N], BF16, name="full")
-            nc.scalar.mul(full[:], dinv_free[:], dinv_lane[:, kb : kb + 1])
-            nc.vector.tensor_tensor(p_sb[:, kb, :], full[:], adj_sb[:, kb, :], ALU.mult)
-
         for t in range(1, LAYERS):
             mix_channels(t, at_half(0))
-            low = mix_channels(t, at_half(1)[:2], LOW_FIRST, WAIT)
-            high = mix_channels(t, at_half(1)[2:], HIGH_FIRST, WAIT)
+            make_p()
+            low = mix_channels(t, at_half(1)[:2], LOW_FIRST)
+            high = mix_channels(t, at_half(1)[2:], HIGH_FIRST)
             keep(low, LOW_FIRST)
             keep(high, HIGH_FIRST)
-            low = spread_nodes(t, at_half(0)[:2], 0, LOW_SECOND, WAIT)
-            high = spread_nodes(t, at_half(0)[2:], 0, HIGH_SECOND, WAIT)
+            low = spread_nodes(t, at_half(0)[:2], 0, LOW_SECOND)
+            high = spread_nodes(t, at_half(0)[2:], 0, HIGH_SECOND)
             keep(low, LOW_SECOND)
             keep(high, HIGH_SECOND)
             spread_nodes(t, at_half(0), 1)
             take_r(t, at_half(0))
+            h0_tenth = reused.tile([LANES, C_BLOCKS, N], F32, name="h0_tenth", tag="rows")
+            for cb in all_blocks:
+                nc.vector.tensor_scalar_mul(h0_tenth[:, cb, :], h0[cb][:], 1.0 / KEPT)
             spread_nodes(t, at_half(1), 0)
             spread_nodes(t, at_half(1), 1)
             take_r(t, at_half(1))
 
         t = LAYERS
-        make_h0_term(0)
         mix_channels(t, [(0, 0), (1, 0)])
-        flipped = mix_channels(t, [(0, 1), (1, 1)], [(0, 0)], WAIT)
+        flipped = mix_channels(t, [(0, 1), (1, 1)], [(0, 0)])
         keep(flipped, [(0, 0)])
-        flipped = spread_nodes(t, [(0, 0), (0, 1)], 0, [(0, 1)], WAIT)
+        flipped = spread_nodes(t, [(0, 0), (0, 1)], 0, [(0, 1)])
         keep(flipped, [(0, 1)])
         flipped = spread_nodes(t, [(0, 0), (0, 1)], 1, [(1, 0), (1, 1)])
         keep(flipped, [(1, 0), (1, 1)])
-        scatter(0)
-        make_h0_term(1)
+        scatter(0, h0_tenth)
         mix_channels(t, [(2, 0), (2, 1)])
-        mix_channels(t, [(3, 0), (3, 1)])
         spread_nodes(t, [(1, 0), (1, 1)], 0)
-        flipped = spread_nodes(t, [(1, 0), (1, 1)], 1, [(2, 0), (2, 1)], LAST)
-        keep(flipped, [(2, 0), (2, 1)])
-        scatter(1)
-        make_h0_term(2)
-        flipped = spread_nodes(t, [(2, 0), (2, 1)], 0, [(3, 0), (3, 1)], WAIT)
-        keep(flipped, [(3, 0), (3, 1)])
-        spread_nodes(t, [(2, 0), (2, 1)], 1)
-        scatter(2)
-        make_h0_term(3)
-        for node_half in range(HALVES):
-            spread_nodes(t, [(3, 0), (3, 1)], node_half)
-        scatter(3)
+        spread_nodes(t, [(1, 0), (1, 1)], 1)
+        scatter(1, h0_tenth)
+        flipped = mix_channels(t, [(3, 0)], [(2, 0)])
+        keep(flipped, [(2, 0)])
+        flipped = spread_nodes(t, [(2, 0), (2, 1)], 0, [(2, 1)])
+        keep(flipped, [(2, 1)])
+        flipped = spread_nodes(t, [(2, 0), (2, 1)], 1, [(3, 0)])
+        keep(flipped, [(3, 0)])
+        scatter(2, h0_tenth)
+        mix_channels(t, [(3, 1)])
+        flipped = spread_nodes(t, [(3, 0), (3, 1)], 0, [(3, 1)])
+        keep(flipped, [(3, 1)])
+        spread_nodes(t, [(3, 0), (3, 1)], 1)
+        scatter(3, h0_tenth)

@@ -71,10 +71,10 @@ def tile_gcnii_b_kernel(tc, x, adj, fc1_w, fc1_b, conv_w, base, offs, out):
             nc.sync.dma_start(windows[cb][:], base[block(cb), :])
         bias = held.tile([LANES, C_BLOCKS], F32, name="bias")
         with nc.allow_non_contiguous_dma(reason="512 bias values, one to a partition"):
-            nc.gpsimd.dma_start(bias[:], fc1_b.rearrange("(cb p) one -> p (cb one)", p=LANES))
+            nc.scalar.dma_start(bias[:], fc1_b.rearrange("(cb p) one -> p (cb one)", p=LANES))
 
         bias_kept = held.tile([LANES, C_BLOCKS], F32, name="bias_kept")
-        nc.vector.tensor_scalar_mul(bias_kept[:], bias[:], ALPHA * KEPT)
+        nc.gpsimd.tensor_scalar_mul(bias_kept[:], bias[:], ALPHA * KEPT)
         identity = held.tile([LANES, LANES], BF16, name="identity")
         make_identity(nc, identity[:])
         identity_f32 = held.tile([LANES, LANES], F32, name="identity_f32")
@@ -143,15 +143,24 @@ def tile_gcnii_b_kernel(tc, x, adj, fc1_w, fc1_b, conv_w, base, offs, out):
         row_sums = held.tile([LANES, N_BLOCKS], F32, name="row_sums")
         dinv_lane = held.tile([LANES, N_BLOCKS], F32, name="dinv_lane")
         rows_sb = reused.tile([LANES, N_BLOCKS, N], BF16, name="rows_sb", tag="rows")
-        for kb in range(N_BLOCKS):
-            nc.vector.tensor_scalar(
-                rows_sb[:, kb, :], adj_sb[:, kb, :], 1.0, None, ALU.mult, ALU.add, accum_out=row_sums[:, kb : kb + 1]
-            )
-            nc.vector.tensor_tensor(adj_sb[:, kb, block(kb)], adj_sb[:, kb, block(kb)], identity[:], ALU.add)
+        for node_half in range(HALVES):
+            kbs = range(node_half * QUARTERS, (node_half + 1) * QUARTERS)
+            for kb in kbs:
+                nc.vector.tensor_scalar(
+                    rows_sb[:, kb, :],
+                    adj_sb[:, kb, :],
+                    1.0,
+                    None,
+                    ALU.mult,
+                    ALU.add,
+                    accum_out=row_sums[:, kb : kb + 1],
+                )
+                nc.vector.tensor_tensor(adj_sb[:, kb, block(kb)], adj_sb[:, kb, block(kb)], identity[:], ALU.add)
             nc.scalar.activation(
-                dinv_lane[:, kb : kb + 1], row_sums[:, kb : kb + 1], ACT.Abs_reciprocal_sqrt, bias=1.0
+                dinv_lane[:, kbs.start : kbs.stop], row_sums[:, kbs.start : kbs.stop], ACT.Abs_reciprocal_sqrt, bias=1.0
             )
-            nc.vector.tensor_scalar_mul(rows_sb[:, kb, :], adj_sb[:, kb, :], dinv_lane[:, kb : kb + 1])
+            for kb in kbs:
+                nc.vector.tensor_scalar_mul(rows_sb[:, kb, :], adj_sb[:, kb, :], dinv_lane[:, kb : kb + 1])
         sums_high = held.tile([LANES, N_BLOCKS], BF16, name="sums_high")
         nc.vector.tensor_copy(sums_high[:], row_sums[:])
         sums_low = held.tile([LANES, N_BLOCKS], BF16, name="sums_low")
@@ -206,10 +215,13 @@ def tile_gcnii_b_kernel(tc, x, adj, fc1_w, fc1_b, conv_w, base, offs, out):
                 )
             return flipped
 
+        def before_p(t, hf):
+            return (t, hf) < (1, 1)
+
         def spread_nodes(t, parts, node_half, flip_parts=(), each=1):
-            moving = rows_sb if t == 0 else p_sb
             matmuls = []
             for cb, hf in parts:
+                moving = rows_sb if before_p(t, hf) else p_sb
                 if node_half == 0:
                     spreads[cb, hf] = banks.tile([LANES, BANK], F32, name="spread", tag="bank")
                 for q in range(QUARTERS):
@@ -230,7 +242,8 @@ def tile_gcnii_b_kernel(tc, x, adj, fc1_w, fc1_b, conv_w, base, offs, out):
                 if hf == 0:
                     r_bf16[t, cb] = layer.tile([LANES, N], BF16, name=f"r_bf16_{cb}")
                     r_kept[t, cb] = layer.tile([LANES, N], F32, name=f"r_kept_{cb}")
-                if t == 0:
+                r = r_kept[t, cb][:, half(hf)] if t == 0 else work.tile([LANES, BANK], F32, name="r")[:]
+                if before_p(t, hf):
                     scaled = work.tile([LANES, BANK], F32, name="scaled")
                     nc.vector.scalar_tensor_tensor(
                         scaled[:],
@@ -240,17 +253,15 @@ def tile_gcnii_b_kernel(tc, x, adj, fc1_w, fc1_b, conv_w, base, offs, out):
                         ALU.mult,
                         ALU.mult,
                     )
-                    r = r_kept[t, cb][:, half(hf)]
                     nc.vector.tensor_tensor(r, scaled[:], h0[cb][:, half(hf)], ALU.add)
-                    nc.scalar.mul(r_bf16[t, cb][:, half(hf)], r, 1.0 / KEPT)
                 else:
-                    r = work.tile([LANES, BANK], F32, name="r")
                     nc.vector.scalar_tensor_tensor(
-                        r[:], spreads[cb, hf][:], (1.0 - ALPHA) * KEPT, h0[cb][:, half(hf)], ALU.mult, ALU.add
+                        r, spreads[cb, hf][:], (1.0 - ALPHA) * KEPT, h0[cb][:, half(hf)], ALU.mult, ALU.add
                     )
-                    nc.scalar.mul(r_bf16[t, cb][:, half(hf)], r[:], 1.0 / KEPT)
+                nc.scalar.mul(r_bf16[t, cb][:, half(hf)], r, 1.0 / KEPT)
+                if t > 0:
                     share = (1.0 - beta(t)) / KEPT / (beta(t) if on_tensor(t, cb) else 1.0)
-                    nc.scalar.mul(r_kept[t, cb][:, half(hf)], r[:], share)
+                    nc.scalar.mul(r_kept[t, cb][:, half(hf)], r, share)
 
         def scatter(cb, h0_tenth):
             term = work.tile([LANES, N], F32, name="term")
@@ -283,7 +294,6 @@ def tile_gcnii_b_kernel(tc, x, adj, fc1_w, fc1_b, conv_w, base, offs, out):
 
         for t in range(1, LAYERS):
             mix_channels(t, at_half(0))
-            make_p()
             low = mix_channels(t, at_half(1)[:2], LOW_FIRST)
             high = mix_channels(t, at_half(1)[2:], HIGH_FIRST)
             keep(low, LOW_FIRST)
@@ -297,6 +307,7 @@ def tile_gcnii_b_kernel(tc, x, adj, fc1_w, fc1_b, conv_w, base, offs, out):
             h0_tenth = reused.tile([LANES, C_BLOCKS, N], F32, name="h0_tenth", tag="rows")
             for cb in all_blocks:
                 nc.vector.tensor_scalar_mul(h0_tenth[:, cb, :], h0[cb][:], 1.0 / KEPT)
+            make_p()
             spread_nodes(t, at_half(1), 0)
             spread_nodes(t, at_half(1), 1)
             take_r(t, at_half(1))

@@ -50,13 +50,20 @@ def tile_gcnii_b_kernel(tc, x, adj, fc1_w, fc1_b, conv_w, base, offs, out):
         tc.psum_pool(name="banks", bufs=6) as banks,
         tc.psum_pool(name="flips", bufs=2) as flips,
     ):
-        fc1_w_sb = held.tile([LANES, C_BLOCKS, C], BF16, name="fc1_w_sb")
-        x_sb = held.tile([LANES, C_BLOCKS, N], BF16, name="x_sb")
-        fc1_w_rows = fc1_w.rearrange("(p ib) c -> p ib c", p=LANES)
-        x_rows = x.rearrange("(p ib) i -> p ib i", p=LANES)
-        for ibs in (slice(0, 1), slice(1, C_BLOCKS)):
-            nc.sync.dma_start(fc1_w_sb[:, ibs, :], fc1_w_rows[:, ibs, :])
-            nc.sync.dma_start(x_sb[:, ibs, :], x_rows[:, ibs, :])
+        fc1_w_flat = held.tile([LANES, C_BLOCKS * C], BF16, name="fc1_w_flat")
+        fc1_w_sb = fc1_w_flat[:].rearrange("p (ib c) -> p ib c", c=C)
+        x_flat = held.tile([LANES, C_BLOCKS * N], BF16, name="x_flat")
+        x_sb = x_flat[:].rearrange("p (ib i) -> p ib i", i=N)
+        fc1_w_rows = fc1_w.rearrange("(p ib) c -> p (ib c)", p=LANES)
+        x_rows = x.rearrange("(p ib) i -> p (ib i)", p=LANES)
+        for rows, flat, cuts in (
+            (x_rows, x_flat, slice(0, BANK)),
+            (fc1_w_rows, fc1_w_flat, slice(0, C // 2)),
+            (fc1_w_rows, fc1_w_flat, slice(C // 2, C_BLOCKS * C)),
+            (x_rows, x_flat, slice(BANK, 2 * N)),
+            (x_rows, x_flat, slice(2 * N, C_BLOCKS * N)),
+        ):
+            nc.sync.dma_start(flat[:, cuts], rows[:, cuts])
         adj_sb = held.tile([LANES, N_BLOCKS, N], BF16, name="adj_sb")
         for kb in range(N_BLOCKS):
             nc.sync.dma_start(adj_sb[:, kb, :], adj[block(kb), :])
@@ -71,7 +78,7 @@ def tile_gcnii_b_kernel(tc, x, adj, fc1_w, fc1_b, conv_w, base, offs, out):
             nc.sync.dma_start(windows[cb][:], base[block(cb), :])
         bias = held.tile([LANES, C_BLOCKS], F32, name="bias")
         with nc.allow_non_contiguous_dma(reason="512 bias values, one to a partition"):
-            nc.scalar.dma_start(bias[:], fc1_b.rearrange("(cb p) one -> p (cb one)", p=LANES))
+            nc.gpsimd.dma_start(bias[:], fc1_b.rearrange("(cb p) one -> p (cb one)", p=LANES))
 
         bias_kept = held.tile([LANES, C_BLOCKS], F32, name="bias_kept")
         nc.gpsimd.tensor_scalar_mul(bias_kept[:], bias[:], ALPHA * KEPT)
@@ -136,15 +143,15 @@ def tile_gcnii_b_kernel(tc, x, adj, fc1_w, fc1_b, conv_w, base, offs, out):
                 low = run(matmuls[8:12], LOW_FIRST, 2)
                 high = run(matmuls[12:], HIGH_FIRST, 2)
                 keep(low, LOW_FIRST, 2)
-                keep(high, HIGH_FIRST)
+                keep(high, HIGH_FIRST, 2)
             for cb in range(C_BLOCKS):
                 keep_h0(cb, hf, products[cb])
 
         row_sums = held.tile([LANES, N_BLOCKS], F32, name="row_sums")
         dinv_lane = held.tile([LANES, N_BLOCKS], F32, name="dinv_lane")
         rows_sb = reused.tile([LANES, N_BLOCKS, N], BF16, name="rows_sb", tag="rows")
-        for node_half in range(HALVES):
-            kbs = range(node_half * QUARTERS, (node_half + 1) * QUARTERS)
+        for first in range(0, N_BLOCKS, 2):
+            kbs = range(first, first + 2)
             for kb in kbs:
                 nc.vector.tensor_scalar(
                     rows_sb[:, kb, :],
@@ -281,8 +288,9 @@ def tile_gcnii_b_kernel(tc, x, adj, fc1_w, fc1_b, conv_w, base, offs, out):
         def at_half(hf):
             return [(cb, hf) for cb in all_blocks]
 
-        low = spread_nodes(0, at_half(0)[:2], 0, LOW_SECOND)
-        high = spread_nodes(0, at_half(0)[2:], 0, HIGH_SECOND)
+        spread_nodes(0, at_half(0)[:1], 0)
+        low = spread_nodes(0, at_half(0)[1:3], 0, LOW_SECOND)
+        high = spread_nodes(0, at_half(0)[3:], 0, HIGH_SECOND, 2)
         keep(low, LOW_SECOND)
         keep(high, HIGH_SECOND)
         degrees_along_free_axis()

@@ -168,10 +168,6 @@ def tile_gcnii_b_kernel(tc, x, adj, fc1_w, fc1_b, conv_w, base, offs, out):
             )
             for kb in kbs:
                 nc.vector.tensor_scalar_mul(rows_sb[:, kb, :], adj_sb[:, kb, :], dinv_lane[:, kb : kb + 1])
-        sums_high = held.tile([LANES, N_BLOCKS], BF16, name="sums_high")
-        nc.vector.tensor_copy(sums_high[:], row_sums[:])
-        sums_low = held.tile([LANES, N_BLOCKS], BF16, name="sums_low")
-        nc.vector.tensor_tensor(sums_low[:], row_sums[:], sums_high[:], ALU.subtract)
         dinv_free = held.tile([LANES, N], F32, name="dinv_free")
 
         def degrees_along_free_axis():
@@ -179,14 +175,8 @@ def tile_gcnii_b_kernel(tc, x, adj, fc1_w, fc1_b, conv_w, base, offs, out):
                 column_sums = banks.tile([LANES, BANK], F32, name="column_sums", tag="bank")
                 for q in range(QUARTERS):
                     kb = hf * QUARTERS + q
-                    for part in (sums_high, sums_low):
-                        nc.tensor.matmul(
-                            column_sums[:, block(q)],
-                            part[:, kb : kb + 1].to_broadcast([LANES, LANES]),
-                            identity[:],
-                            start=(part is sums_high),
-                            stop=(part is sums_low),
-                        )
+                    same_columns = row_sums[:, kb : kb + 1].to_broadcast([LANES, LANES])
+                    nc.tensor.transpose(column_sums[:, block(q)], same_columns, identity_f32[:])
                 nc.scalar.activation(dinv_free[:, half(hf)], column_sums[:], ACT.Abs_reciprocal_sqrt, bias=1.0)
 
         r_bf16 = {}
@@ -326,10 +316,11 @@ def tile_gcnii_b_kernel(tc, x, adj, fc1_w, fc1_b, conv_w, base, offs, out):
         keep(flipped, [(0, 0)])
         flipped = spread_nodes(t, [(0, 0), (0, 1)], 0, [(0, 1)])
         keep(flipped, [(0, 1)])
-        flipped = spread_nodes(t, [(0, 0), (0, 1)], 1, [(1, 0), (1, 1)])
-        keep(flipped, [(1, 0), (1, 1)])
+        flipped = spread_nodes(t, [(0, 0), (0, 1)], 1, [(1, 0)])
         scatter(0, h0_tenth)
-        mix_channels(t, [(2, 0), (2, 1)])
+        keep(flipped, [(1, 0)])
+        flipped = mix_channels(t, [(2, 0), (2, 1)], [(1, 1)])
+        keep(flipped, [(1, 1)])
         spread_nodes(t, [(1, 0), (1, 1)], 0)
         spread_nodes(t, [(1, 0), (1, 1)], 1)
         scatter(1, h0_tenth)

@@ -105,12 +105,15 @@ def tile_gcnii_b_kernel(tc, x, adj, fc1_w, fc1_b, conv_w, base, offs, out):
                     nc.tensor.transpose(flipped[:, block(j * QUARTERS + q)], pre[part][:, block(q)], identity[:])
             return flipped
 
-        def keep(flipped, parts, pieces=1):
+        def keep(flipped, parts, pieces=1, on_vector=False):
             nodes_first = states.tile([LANES, N], BF16, name="nodes_first")
             width = len(parts) * BANK // pieces
             for piece in range(pieces):
                 cut = slice(piece * width, (piece + 1) * width)
-                nc.scalar.activation(nodes_first[:, cut], flipped[:, cut], ACT.Relu)
+                if on_vector:
+                    nc.vector.tensor_scalar_max(nodes_first[:, cut], flipped[:, cut], 0.0)
+                else:
+                    nc.scalar.activation(nodes_first[:, cut], flipped[:, cut], ACT.Relu)
             for j, part in enumerate(parts):
                 h_nodes[part] = nodes_first[:, half(j)]
 
@@ -281,8 +284,8 @@ def tile_gcnii_b_kernel(tc, x, adj, fc1_w, fc1_b, conv_w, base, offs, out):
         spread_nodes(0, at_half(0)[:1], 0)
         low = spread_nodes(0, at_half(0)[1:3], 0, LOW_SECOND)
         high = spread_nodes(0, at_half(0)[3:], 0, HIGH_SECOND, 2)
-        keep(low, LOW_SECOND)
-        keep(high, HIGH_SECOND)
+        keep(low, LOW_SECOND, on_vector=True)
+        keep(high, HIGH_SECOND, on_vector=True)
         degrees_along_free_axis()
         spread_nodes(0, at_half(0), 1)
         take_r(0, at_half(0))

import math

import concourse.mybir as mybir
from concourse.masks import make_identity

F32, BF16, U16 = mybir.dt.float32, mybir.dt.bfloat16, mybir.dt.uint16
ALU = mybir.AluOpType
ACT = mybir.ActivationFunctionType

LANES = 128
F, C, S, N = 512, 512, 2048, 1024
LAYERS = 2
ALPHA, LAMDA = 0.1, 0.5
BANK = 512
C_BLOCKS, N_BLOCKS = C // LANES, N // LANES
HALVES = N // BANK
QUARTERS = BANK // LANES
LOW_FIRST, LOW_SECOND = ((0, 0), (1, 0)), ((0, 1), (1, 1))
HIGH_FIRST, HIGH_SECOND = ((2, 0), (3, 0)), ((2, 1), (3, 1))
assert F == C

FLOPS = 2 * N * (F * C + LAYERS * C * C + (LAYERS + 1) * C * N)


def beta(t):
    return math.log(LAMDA / (t + 1) + 1.0)


KEPT = 1.0 - beta(0)


def block(b):
    return slice(b * LANES, (b + 1) * LANES)


def half(hf):
    return slice(hf * BANK, (hf + 1) * BANK)


def tile_gcnii_b_kernel(tc, x, adj, fc1_w, fc1_b, conv_w, base, offs, out):
    nc = tc.nc
    with (
        tc.tile_pool(name="lists", bufs=1) as lists,
        tc.tile_pool(name="held", bufs=1) as held,
        tc.tile_pool(name="reused", bufs=1) as reused,
        tc.tile_pool(name="layer", bufs=2) as layer,
        tc.tile_pool(name="work", bufs=3) as work,
        tc.tile_pool(name="parts", bufs=10) as parts_pool,
        tc.tile_pool(name="states", bufs=5) as states,
        tc.psum_pool(name="banks", bufs=6) as banks,
        tc.psum_pool(name="flips", bufs=2) as flips,
    ):
        fc1_w_flat = held.tile([LANES, C_BLOCKS * C], BF16, name="fc1_w_flat")
        fc1_w_sb = fc1_w_flat[:].rearrange("p (ib c) -> p ib c", c=C)
        x_flat = held.tile([LANES, C_BLOCKS * N], BF16, name="x_flat")
        x_sb = x_flat[:].rearrange("p (ib i) -> p ib i", i=N)
        fc1_w_rows = fc1_w.rearrange("(p ib) c -> p (ib c)", p=LANES)
        x_rows = x.rearrange("(p ib) i -> p (ib i)", p=LANES)
        for rows, flat, cuts in (
            (x_rows, x_flat, slice(0, BANK)),
            (fc1_w_rows, fc1_w_flat, slice(0, C // 2)),
            (fc1_w_rows, fc1_w_flat, slice(C // 2, C_BLOCKS * C)),
            (x_rows, x_flat, slice(BANK, 2 * N)),
            (x_rows, x_flat, slice(2 * N, C_BLOCKS * N)),
        ):
            nc.sync.dma_start(flat[:, cuts], rows[:, cuts])
        adj_sb = held.tile([LANES, N_BLOCKS, N], BF16, name="adj_sb")
        for kb in range(N_BLOCKS):
            nc.sync.dma_start(adj_sb[:, kb, :], adj[block(kb), :])
        conv_w_sb = held.tile([LANES, LAYERS, C_BLOCKS, C], BF16, name="conv_w_sb")
        for t in range(LAYERS):
            for ib in range(C_BLOCKS):
                nc.sync.dma_start(conv_w_sb[:, t, ib, :], conv_w[t, block(ib), :])
        offsets = lists.tile([LANES, N // 16], U16, name="offsets")
        nc.sync.dma_start(offsets[:], offs)
        windows = [held.tile([LANES, S], F32, name=f"window{cb}") for cb in range(C_BLOCKS)]
        for cb in range(C_BLOCKS):
            nc.sync.dma_start(windows[cb][:], base[block(cb), :])
        bias = held.tile([LANES, C_BLOCKS], F32, name="bias")
        with nc.allow_non_contiguous_dma(reason="512 bias values, one to a partition"):
            nc.gpsimd.dma_start(bias[:], fc1_b.rearrange("(cb p) one -> p (cb one)", p=LANES))

        bias_kept = held.tile([LANES, C_BLOCKS], F32, name="bias_kept")
        nc.gpsimd.tensor_scalar_mul(bias_kept[:], bias[:], ALPHA * KEPT)
        identity = held.tile([LANES, LANES], BF16, name="identity")
        make_identity(nc, identity[:])
        identity_f32 = held.tile([LANES, LANES], F32, name="identity_f32")
        make_identity(nc, identity_f32[:])
        one = held.tile([LANES, 1], F32, name="one")
        nc.vector.memset(one[:], 1.0)
        nc.scalar.activation(one[:], one[:], ACT.Abs_reciprocal_sqrt)

        h0 = [held.tile([LANES, N], F32, name=f"h0_{cb}") for cb in range(C_BLOCKS)]
        pre = {}
        h_nodes = {}
        spreads = {}

        def run(matmuls, parts=(), each=1):
            flipped = flips.tile([LANES, N], BF16, name="flipped") if parts else None
            blocks = [(j, part, q) for j, part in enumerate(parts) for q in range(QUARTERS)]
            for n, (product, stationary, moving, start, stop) in enumerate(matmuls):
                nc.tensor.matmul(product, stationary, moving, start=start, stop=stop)
                due = each * n + each if n < len(matmuls) - 1 else len(blocks)
                for j, part, q in blocks[each * n : due]:
                    nc.tensor.transpose(flipped[:, block(j * QUARTERS + q)], pre[part][:, block(q)], identity[:])
            return flipped

        def keep(flipped, parts, pieces=1, on_vector=False):
            nodes_first = states.tile([LANES, N], BF16, name="nodes_first")
            width = len(parts) * BANK // pieces
            for piece in range(pieces):
                cut = slice(piece * width, (piece + 1) * width)
                if on_vector:
                    nc.vector.tensor_scalar_max(nodes_first[:, cut], flipped[:, cut], 0.0)
                else:
                    nc.scalar.activation(nodes_first[:, cut], flipped[:, cut], ACT.Relu)
            for j, part in enumerate(parts):
                h_nodes[part] = nodes_first[:, half(j)]

        def keep_h0(cb, hf, product):
            nc.scalar.activation(
                h0[cb][:, half(hf)], product[:], ACT.Relu, bias=bias_kept[:, cb : cb + 1], scale=ALPHA * KEPT
            )
            pre[cb, hf] = parts_pool.tile([LANES, BANK], BF16, name="pre")
            nc.vector.tensor_scalar_mul(pre[cb, hf][:], h0[cb][:, half(hf)], 1.0 / (ALPHA * KEPT))

        for hf in range(HALVES):
            products = [banks.tile([LANES, BANK], F32, name=f"product{cb}", tag="bank") for cb in range(C_BLOCKS)]
            order = [(cb, ib) for ib in range(C_BLOCKS) for cb in range(C_BLOCKS)]
            if hf == 1:
                order = [(cb, ib) for cb in range(C_BLOCKS) for ib in range(C_BLOCKS)]
            matmuls = [
                (
                    products[cb][:],
                    fc1_w_sb[:, ib, block(cb)],
                    x_sb[:, ib, half(hf)],
                    ib == 0,
                    ib == C_BLOCKS - 1,
                )
                for cb, ib in order
            ]
            if hf == 0:
                run(matmuls)
            else:
                run(matmuls[:8])
                low = run(matmuls[8:12], LOW_FIRST, 2)
                high = run(matmuls[12:], HIGH_FIRST, 2)
                keep(low, LOW_FIRST, 2)
                keep(high, HIGH_FIRST, 2)
            for cb in range(C_BLOCKS):
                keep_h0(cb, hf, products[cb])

        row_sums = held.tile([LANES, N_BLOCKS], F32, name="row_sums")
        dinv_lane = held.tile([LANES, N_BLOCKS], F32, name="dinv_lane")
        rows_sb = reused.tile([LANES, N_BLOCKS, N], BF16, name="rows_sb", tag="rows")
        for first in range(0, N_BLOCKS, 2):
            kbs = range(first, first + 2)
            for kb in kbs:
                nc.vector.tensor_scalar(
                    rows_sb[:, kb, :],
                    adj_sb[:, kb, :],
                    1.0,
                    None,
                    ALU.mult,
                    ALU.add,
                    accum_out=row_sums[:, kb : kb + 1],
                )
                nc.vector.tensor_tensor(adj_sb[:, kb, block(kb)], adj_sb[:, kb, block(kb)], identity[:], ALU.add)
            nc.scalar.activation(
                dinv_lane[:, kbs.start : kbs.stop], row_sums[:, kbs.start : kbs.stop], ACT.Abs_reciprocal_sqrt, bias=1.0
            )
            for kb in kbs:
                nc.vector.tensor_scalar_mul(rows_sb[:, kb, :], adj_sb[:, kb, :], dinv_lane[:, kb : kb + 1])
        dinv_free = held.tile([LANES, N], F32, name="dinv_free")

        def degrees_along_free_axis():
            for hf in range(HALVES):
                column_sums = banks.tile([LANES, BANK], F32, name="column_sums", tag="bank")
                for q in range(QUARTERS):
                    kb = hf * QUARTERS + q
                    same_columns = row_sums[:, kb : kb + 1].to_broadcast([LANES, LANES])
                    nc.tensor.transpose(column_sums[:, block(q)], same_columns, identity_f32[:])
                nc.scalar.activation(dinv_free[:, half(hf)], column_sums[:], ACT.Abs_reciprocal_sqrt, bias=1.0)

        r_bf16 = {}
        r_kept = {}
        p_sb = held.tile([LANES, N_BLOCKS, N], BF16, name="p_sb")

        def on_tensor(t, cb):
            return t == LAYERS - 1 and cb == C_BLOCKS - 1

        def mix_channels(t, parts, flip_parts=(), each=1):
            products = {part: banks.tile([LANES, BANK], F32, name="product", tag="bank") for part in parts}
            matmuls = []
            for cb, hf in parts:
                for ib in range(C_BLOCKS):
                    stationary, moving = conv_w_sb[:, t - 1, ib, block(cb)], r_bf16[t - 1, ib][:, half(hf)]
                    stop = ib == C_BLOCKS - 1 and not on_tensor(t - 1, cb)
                    matmuls.append((products[cb, hf][:], stationary, moving, ib == 0, stop))
                if on_tensor(t - 1, cb):
                    matmuls.append((products[cb, hf][:], identity_f32[:], r_kept[t - 1, cb][:, half(hf)], False, True))
            flipped = run(matmuls, flip_parts, each)
            for cb, hf in parts:
                pre[cb, hf] = parts_pool.tile([LANES, BANK], BF16, name="pre")
                if on_tensor(t - 1, cb):
                    nc.scalar.mul(pre[cb, hf][:], products[cb, hf][:], beta(t - 1))
                    continue
                nc.vector.scalar_tensor_tensor(
                    pre[cb, hf][:],
                    products[cb, hf][:],
                    beta(t - 1),
                    r_kept[t - 1, cb][:, half(hf)],
                    ALU.mult,
                    ALU.add,
                )
            return flipped

        def before_p(t, hf):
            return (t, hf) < (1, 1)

        def spread_nodes(t, parts, node_half, flip_parts=(), each=1):
            matmuls = []
            for cb, hf in parts:
                moving = rows_sb if before_p(t, hf) else p_sb
                if node_half == 0:
                    spreads[cb, hf] = banks.tile([LANES, BANK], F32, name="spread", tag="bank")
                for q in range(QUARTERS):
                    kb = node_half * QUARTERS + q
                    matmuls.append(
                        (
                            spreads[cb, hf][:],
                            h_nodes[cb, node_half][:, block(q)],
                            moving[:, kb, half(hf)],
                            kb == 0,
                            kb == N_BLOCKS - 1,
                        )
                    )
            return run(matmuls, flip_parts, each)

        def take_r(t, parts):
            for cb, hf in parts:
                if hf == 0:
                    r_bf16[t, cb] = layer.tile([LANES, N], BF16, name=f"r_bf16_{cb}")
                    r_kept[t, cb] = layer.tile([LANES, N], F32, name=f"r_kept_{cb}")
                r = r_kept[t, cb][:, half(hf)] if t == 0 else work.tile([LANES, BANK], F32, name="r")[:]
                if before_p(t, hf):
                    scaled = work.tile([LANES, BANK], F32, name="scaled")
                    nc.vector.scalar_tensor_tensor(
                        scaled[:],
                        spreads[cb, hf][:],
                        (1.0 - ALPHA) * KEPT,
                        dinv_free[:, half(hf)],
                        ALU.mult,
                        ALU.mult,
                    )
                    nc.vector.tensor_tensor(r, scaled[:], h0[cb][:, half(hf)], ALU.add)
                else:
                    nc.vector.scalar_tensor_tensor(
                        r, spreads[cb, hf][:], (1.0 - ALPHA) * KEPT, h0[cb][:, half(hf)], ALU.mult, ALU.add
                    )
                nc.scalar.mul(r_bf16[t, cb][:, half(hf)], r, 1.0 / KEPT)
                if t > 0:
                    share = (1.0 - beta(t)) / KEPT / (beta(t) if on_tensor(t, cb) else 1.0)
                    nc.scalar.mul(r_kept[t, cb][:, half(hf)], r, share)

        def scatter(cb, h0_tenth):
            term = work.tile([LANES, N], F32, name="term")
            for hf in range(HALVES):
                nc.scalar.mul(term[:, half(hf)], spreads[cb, hf][:], 1.0 - ALPHA)
            nc.vector.tensor_tensor(windows[cb][:].indirect(offsets[:]), term[:], h0_tenth[:, cb, :], ALU.add)
            nc.sync.dma_start(out[block(cb), :], windows[cb][:])

        def make_p():
            for kb in range(N_BLOCKS):
                full = work.tile([LANES, N], BF16, name="full")
                nc.scalar.mul(full[:], dinv_free[:], dinv_lane[:, kb : kb + 1])
                nc.vector.tensor_tensor(p_sb[:, kb, :], full[:], adj_sb[:, kb, :], ALU.mult)

        all_blocks = range(C_BLOCKS)

        def at_half(hf):
            return [(cb, hf) for cb in all_blocks]

        spread_nodes(0, at_half(0)[:1], 0)
        low = spread_nodes(0, at_half(0)[1:3], 0, LOW_SECOND)
        high = spread_nodes(0, at_half(0)[3:], 0, HIGH_SECOND, 2)
        keep(low, LOW_SECOND, on_vector=True)
        keep(high, HIGH_SECOND, on_vector=True)
        degrees_along_free_axis()
        spread_nodes(0, at_half(0), 1)
        take_r(0, at_half(0))
        spread_nodes(0, at_half(1), 0)
        spread_nodes(0, at_half(1), 1)
        take_r(0, at_half(1))

        for t in range(1, LAYERS):
            mix_channels(t, at_half(0))
            low = mix_channels(t, at_half(1)[:2], LOW_FIRST)
            high = mix_channels(t, at_half(1)[2:], HIGH_FIRST)
            keep(low, LOW_FIRST)
            keep(high, HIGH_FIRST)
            low = spread_nodes(t, at_half(0)[:2], 0, LOW_SECOND)
            high = spread_nodes(t, at_half(0)[2:], 0, HIGH_SECOND)
            keep(low, LOW_SECOND)
            keep(high, HIGH_SECOND)
            spread_nodes(t, at_half(0), 1)
            take_r(t, at_half(0))
            h0_tenth = reused.tile([LANES, C_BLOCKS, N], F32, name="h0_tenth", tag="rows")
            for cb in all_blocks:
                nc.vector.tensor_scalar_mul(h0_tenth[:, cb, :], h0[cb][:], 1.0 / KEPT)
            make_p()
            spread_nodes(t, at_half(1), 0)
            spread_nodes(t, at_half(1), 1)
            take_r(t, at_half(1))

        t = LAYERS
        mix_channels(t, [(0, 0), (1, 0)])
        flipped = mix_channels(t, [(0, 1), (1, 1)], [(0, 0)])
        keep(flipped, [(0, 0)])
        flipped = spread_nodes(t, [(0, 0), (0, 1)], 0, [(0, 1)])
        keep(flipped, [(0, 1)])
        flipped = spread_nodes(t, [(0, 0), (0, 1)], 1, [(1, 0)])
        scatter(0, h0_tenth)
        keep(flipped, [(1, 0)])
        flipped = mix_channels(t, [(2, 0), (2, 1)], [(1, 1)])
        keep(flipped, [(1, 1)])
        spread_nodes(t, [(1, 0), (1, 1)], 0)
        spread_nodes(t, [(1, 0), (1, 1)], 1)
        scatter(1, h0_tenth)
        flipped = mix_channels(t, [(3, 0)], [(2, 0)])
        keep(flipped, [(2, 0)])
        flipped = spread_nodes(t, [(2, 0), (2, 1)], 0, [(2, 1)])
        keep(flipped, [(2, 1)])
        flipped = spread_nodes(t, [(2, 0), (2, 1)], 1, [(3, 0)])
        keep(flipped, [(3, 0)])
        scatter(2, h0_tenth)
        mix_channels(t, [(3, 1)])
        flipped = spread_nodes(t, [(3, 0), (3, 1)], 0, [(3, 1)])
        keep(flipped, [(3, 1)])
        spread_nodes(t, [(3, 0), (3, 1)], 1)
        scatter(3, h0_tenth)
